import numpy as np
import ml_dtypes


def mxq(x, axis, fmt="e4m3"):
    dtype, down = {"e4m3": (ml_dtypes.float8_e4m3fn, 7), "e5m2": (ml_dtypes.float8_e5m2, 14)}[fmt]
    v = np.moveaxis(np.asarray(x, np.float32).astype(ml_dtypes.bfloat16).astype(np.float64), axis, -1)
    blocks = v.reshape(v.shape[:-1] + (-1, 32))
    amax = np.abs(blocks).max(-1, keepdims=True)
    byte = np.maximum(np.where(amax > 0, np.frexp(amax)[1] - 1 + 127, 0) - down, 1)
    scale = np.exp2(byte - 127.0)
    codes = (blocks / scale).astype(np.float32).astype(dtype).astype(np.float64)
    return np.moveaxis((codes * scale).reshape(v.shape), -1, axis)


WIDE = False


def mx_kscale(k):
    if not WIDE:
        return np.ones(k)
    levels = np.array([18, -18])
    if k % 512:
        return np.exp2(np.random.permutation(np.resize(levels, k // 32))).repeat(32)
    a = np.empty((k // 512, 16))
    for p in range(k // 512):
        a[p, :8] = np.random.permutation(np.resize(levels, 8))
        for g in range(8):
            far = levels[np.abs(levels - a[p, g]) >= 10]
            a[p, g + 8] = far[np.random.randint(len(far))]
    return np.exp2(a.ravel()).repeat(32)


BF16 = ml_dtypes.bfloat16


def bf(x):
    return np.asarray(x, np.float32).astype(BF16)


def f64(x):
    return np.asarray(x).astype(np.float64)


B, F, DEPTH, T, DO = 1024, 512, 4, 256, 512
L = 2 ** DEPTH
H = T * DEPTH


def sigmoid(v):
    return 1.0 / (1.0 + np.exp(-v))


def pre_activation(x, W, b):
    return np.matmul(f64(x), f64(W)).transpose(1, 0, 2) + f64(b)


def setup_inputs():
    s = mx_kscale(B)[:, None]
    u = mx_kscale(DO)
    vt = mx_kscale(H).reshape(T, DEPTH)[:, 0]
    x0 = bf(np.random.standard_normal((B, F)))
    W0 = bf(np.random.standard_normal((DEPTH, F, T)) * 1.5 / np.sqrt(F))
    b = bf(np.random.standard_normal((DEPTH, T)) * 0.5)
    leaf0 = bf(np.random.standard_normal((T, L, DO)) * np.sqrt(T))
    g = bf(np.random.standard_normal((B, DO)) * np.exp2(np.random.randint(-6, 1, (B, 1))) * 8.0 / s * u)
    z = pre_activation(x0, W0, b)
    return {"x": bf(f64(x0) * s),
            "W": bf(f64(W0) / vt),
            "b": b,
            "leaf_values": bf(f64(leaf0) * vt[:, None, None] / u),
            "z": np.ascontiguousarray(z, np.float32),
            "grad_out": g}


def reference(x, W, b, leaf_values, z, grad_out):
    n = x.shape[0]
    p = sigmoid(f64(z))
    q = 1.0 - p
    gq = mxq(f64(grad_out), 1, "e5m2")
    lq = mxq(f64(leaf_values).reshape(T * L, DO), 1, "e4m3")
    dpath = ((gq @ lq.T) / T).reshape(n, T, L)
    dz = []
    for j in range(DEPTH):
        a = dpath
        for k in range(DEPTH - 1, -1, -1):
            a = a.reshape(n, T, 2 ** k, 2)
            if k == j:
                a = a[..., 0] - a[..., 1]
            else:
                a = a[..., 0] * p[:, k, :, None] + a[..., 1] * q[:, k, :, None]
        dz.append(a[..., 0] * p[:, j] * q[:, j])
    dz1 = np.stack(dz, axis=2).reshape(n, H)
    wq = mxq(f64(W).transpose(1, 2, 0).reshape(F, H), 1, "e4m3")
    dx = mxq(dz1, 1, "e5m2") @ wq.T
    dw = mxq(f64(x), 0, "e4m3").T @ mxq(dz1, 0, "e5m2")
    return dx, dw.reshape(F, T, DEPTH).transpose(2, 0, 1)

@@ -1,0 +1,328 @@
+from contextlib import ExitStack
+
+import concourse.mybir as mybir
+from concourse.masks import make_identity
+
+B, F, DEPTH, T, DO = 1024, 512, 4, 256, 512
+L = 2 ** DEPTH
+H = T * DEPTH
+
+FLOPS = 2 * B * DO * T * L + 2 * 2 * B * F * H
+BYTES = 2 * B * F + 2 * F * H + 2 * T * L * DO + 4 * B * H + 2 * B * DO + 4 * B * F + 4 * F * H
+
+F32 = mybir.dt.float32
+BF16 = mybir.dt.bfloat16
+U32 = mybir.dt.uint32
+U8 = mybir.dt.uint8
+E4 = mybir.dt.float8_e4m3fn_x4
+E5 = mybir.dt.float8_e5m2_x4
+ALU = mybir.AluOpType
+ACT = mybir.ActivationFunctionType
+
+P = 128
+PACK = 4
+NB = B // (P * PACK)
+TB = T // P
+INV_T = 1.0 / T
+
+
+def tile_neuralobliviousdecisiontree_v_kernel(tc, x, W, b, leaf_values, z, grad_out, out_0, out_1):
+    nc = tc.nc
+    with ExitStack() as ctx:
+        const = ctx.enter_context(tc.tile_pool(name="const", bufs=1))
+        raw = ctx.enter_context(tc.tile_pool(name="raw", bufs=8))
+        work = ctx.enter_context(tc.tile_pool(name="work", bufs=2))
+        psum = ctx.enter_context(tc.psum_pool(name="psum", bufs=2))
+
+        ident_f = const.tile([P, P], F32, name="ident_f")
+        make_identity(nc, ident_f[:])
+        ident_b = const.tile([P, P], BF16, name="ident_b")
+        make_identity(nc, ident_b[:])
+
+        def codes_tile(name, cols):
+            c = const.tile([P, cols], U32, name=name + "_c", align_bytes=64)
+            s = const.tile([P, cols], U8, name=name + "_s", align_bytes=64)
+            return c, s
+
+        leaf_q = [codes_tile("leaf%d" % tb, L * P) for tb in range(TB)]
+        gpos_q = [codes_tile("gpos%d" % nb, 512) for nb in range(NB)]
+        gneg_q = [codes_tile("gneg%d" % nb, 512) for nb in range(NB)]
+        x_q = [codes_tile("x%d" % nb, F) for nb in range(NB)]
+        w_q = [codes_tile("w%d" % tb, F) for tb in range(TB)]
+        tok_q = [[codes_tile("tok%d%d" % (tb, nb), 512) for nb in range(NB)] for tb in range(TB)]
+        feat_q = [[codes_tile("feat%d%d" % (tb, nb), 512) for nb in range(NB)] for tb in range(TB)]
+
+        z_v = z.rearrange("n l t -> (n l) t").rearrange("(g p m) t -> p g m t", p=P, m=PACK * DEPTH)
+        g_v = grad_out.rearrange("(g p j) d -> p g j d", p=P, j=PACK)
+        x_v = x.rearrange("(g p j) f -> p g j f", p=P, j=PACK)
+        o0_v = out_0.rearrange("(g p j) f -> p g j f", p=P, j=PACK)
+        w_v = W.rearrange("l (b p) t -> p b l t", p=P)
+        o1_v = out_1.rearrange("l f t -> f l t")
+
+        def load_z(tb, nb):
+            tiles = []
+            for h in range(2):
+                t = raw.tile([P, 2 * DEPTH, P], F32, name="raw", tag="raw")
+                nc.sync.dma_start(out=t[:], in_=z_v[:, nb, 8 * h:8 * h + 8, tb * P:(tb + 1) * P])
+                tiles.append(t)
+            return tiles
+
+        def load_g(nb):
+            t = raw.tile([P, PACK, DO], BF16, name="raw", tag="raw")
+            nc.sync.dma_start(out=t[:], in_=g_v[:, nb, :, :])
+            return t
+
+        def load_leaf(tb, q):
+            t = raw.tile([P, 4, DO], BF16, name="raw", tag="raw")
+            nc.sync.dma_start(out=t[:], in_=leaf_values[tb * P:(tb + 1) * P, 4 * q:4 * q + 4, :])
+            return t
+
+        def load_x(nb):
+            t = raw.tile([P, PACK, F], BF16, name="raw", tag="raw")
+            nc.sync.dma_start(out=t[:], in_=x_v[:, nb, :, :])
+            return t
+
+        def load_w(half):
+            t = raw.tile([P, 2, DEPTH, T], BF16, name="raw", tag="raw")
+            for i in range(2):
+                nc.sync.dma_start(out=t[:, i, :, :], in_=w_v[:, 2 * half + i, :, :])
+            return t
+
+        def quantize(q, cols, src, fmt):
+            nc.vector.quantize_mx(out=q[0][:, cols].bitcast(fmt), scales=q[1][:, cols], in_=src)
+
+        def words_bank(src_a, src_b):
+            bank = psum.tile([P, 2, 2, P], F32, name="tr", tag="tr", bufs=2)
+            for i, s in enumerate((src_a, src_b)):
+                words = s.bitcast(F32)
+                for u in range(2):
+                    nc.tensor.transpose(bank[:, i, u, :], words[:, u:256:2], ident_f[:])
+            return bank
+
+        def prep_leaf(tb, q, t, engines):
+            for i in range(2):
+                bank = words_bank(t[:, 2 * i, :], t[:, 2 * i + 1, :])
+                grp = work.tile([P, 2 * P * PACK], BF16, name="lgrp", tag="lgrp", bufs=4, align_bytes=64)
+                dst = grp[:].bitcast(F32).rearrange("k (i p u) -> k i p u", i=2, u=2)
+                src = bank[:].rearrange("k i u p -> k i p u")
+                if engines[i] == "v":
+                    nc.vector.tensor_copy(out=dst, in_=src)
+                else:
+                    nc.scalar.copy(out=dst, in_=src)
+                l0 = 4 * q + 2 * i
+                quantize(leaf_q[tb], slice(l0 * P, (l0 + 2) * P), grp[:], E4)
+
+        def prep_g(nb, t):
+            grp = work.tile([P, 2048], BF16, name="grp", tag="grp", bufs=4, align_bytes=64)
+            for i in range(2):
+                bank = words_bank(t[:, 2 * i, :], t[:, 2 * i + 1, :])
+                dst = grp[:, 1024 * i:1024 * (i + 1)].bitcast(F32).rearrange("k (i p u) -> k i p u", i=2, u=2)
+                nc.scalar.copy(out=dst, in_=bank[:].rearrange("k i u p -> k i p u"))
+            neg = work.tile([P, 2048], BF16, name="grp", tag="grp", bufs=4, align_bytes=64)
+            nc.vector.tensor_scalar_mul(neg[:], grp[:], -1.0)
+            quantize(gpos_q[nb], slice(0, 512), grp[:], E5)
+            quantize(gneg_q[nb], slice(0, 512), neg[:], E5)
+
+        def interleave(dst, src):
+            nc.scalar.copy(out=dst.rearrange("p (c i) t -> p c t i", i=4), in_=src.rearrange("p t (c i) -> p c t i", i=4))
+
+        def prep_x(nb, t):
+            grp = work.tile([P, 2048], BF16, name="grp", tag="grp", bufs=4, align_bytes=64)
+            interleave(grp[:].rearrange("p (c t) -> p c t", t=4), t[:])
+            quantize(x_q[nb], slice(0, F), grp[:], E4)
+
+        def prep_w(tb, halves):
+            grp = work.tile([P, 2048], BF16, name="grp", tag="grp", bufs=4, align_bytes=64)
+            for fb in range(4):
+                bank = psum.tile([P, DEPTH, P], BF16, name="tr", tag="tr", bufs=2)
+                for lev in range(DEPTH):
+                    nc.tensor.transpose(bank[:, lev, :], halves[fb // 2][:, fb % 2, lev, tb * P:(tb + 1) * P], ident_b[:])
+                nc.scalar.copy(out=grp[:, 512 * fb:512 * (fb + 1)].rearrange("t (f l) -> t f l", l=DEPTH),
+                               in_=bank[:].rearrange("t l f -> t f l"))
+            quantize(w_q[tb], slice(0, F), grp[:], E4)
+
+        def prep_p(c, rz):
+            pq = []
+            for lev in range(3):
+                bank = psum.tile([P, 512], F32, name="tr", tag="tr", bufs=2)
+                for j in range(PACK):
+                    nc.tensor.transpose(bank[:, j * P:(j + 1) * P], rz[j // 2][:, (j % 2) * DEPTH + lev, :], ident_f[:])
+                t = work.tile([P, 2, 512], F32, name="pq%d" % lev, tag="pq%d" % lev, bufs=1)
+                nc.scalar.activation(out=t[:, 1, :], in_=bank[:], func=ACT.Sigmoid)
+                nc.scalar.activation(out=t[:, 0, :], in_=bank[:], func=ACT.Sigmoid, scale=-1.0)
+                pq.append(t)
+            ptok, stok = [], []
+            for h in range(2):
+                pt = work.tile([P, 2, DEPTH, P], F32, name="ptok", tag="ptok", bufs=3)
+                nc.scalar.activation(out=pt[:].rearrange("p j l t -> p (j l) t"), in_=rz[h][:], func=ACT.Sigmoid)
+                qw = work.tile([P, 2, P], F32, name="qw", tag="qw", bufs=2)
+                nc.scalar.activation(out=qw[:], in_=rz[h][:, 3:2 * DEPTH:DEPTH, :], func=ACT.Sigmoid, scale=-1.0)
+                st = work.tile([P, 2, P], F32, name="stok", tag="stok", bufs=3)
+                nc.gpsimd.tensor_tensor(out=st[:], in0=pt[:, :, 3, :], in1=qw[:], op=ALU.mult)
+                ptok.append(pt)
+                stok.append(st)
+            pi = {}
+            for bx in (1, 0):
+                for by in (1, 0):
+                    al = work.tile([P, 512], F32, name="alpha", tag="alpha", bufs=3)
+                    eng = nc.vector if c == 0 else nc.gpsimd
+                    eng.tensor_tensor(out=al[:], in0=pq[0][:, bx, :], in1=pq[1][:, by, :], op=ALU.mult)
+                    for bz in (0, 1):
+                        w_ = work.tile([P, 512], F32, name="pi", tag="pi", bufs=11)
+                        eng2 = nc.vector if (c == 0 and bz == 0) else nc.gpsimd
+                        eng2.tensor_tensor(out=w_[:], in0=al[:], in1=pq[2][:, bz, :], op=ALU.mult)
+                        pi[bx, by, bz] = w_
+            return pi, ptok, stok
+
+        def mx_pass(out, tb, l, gq, start, stop):
+            nc.tensor.matmul_mx(out=out, lhsT=leaf_q[tb][0][:, l * P:(l + 1) * P].bitcast(E4),
+                                lhsT_scale=leaf_q[tb][1][:, l * P:(l + 1) * P],
+                                rhs=gq[0][:].bitcast(E5), rhs_scale=gq[1][:], start=start, stop=stop)
+
+        def stage_one(tb, nb, pi):
+            kap, nup, nus = {}, {}, {}
+            for bx in (1, 0):
+                for by in (1, 0):
+                    nq = None
+                    for bz in (0, 1):
+                        l0 = 8 * (1 - bx) + 4 * (1 - by) + 2 * (1 - bz)
+                        wt = pi[bx, by, bz]
+                        dmm = psum.tile([P, 512], F32, name="mm", tag="mm", bufs=3)
+                        mx_pass(dmm[:], tb, l0, gpos_q[nb], True, False)
+                        mx_pass(dmm[:], tb, l0 + 1, gneg_q[nb], False, True)
+                        k_ = work.tile([P, 512], F32, name="kap", tag="kap", bufs=8)
+                        nc.vector.tensor_tensor(out=k_[:], in0=dmm[:], in1=wt[:], op=ALU.mult)
+                        kap[bx, by, bz] = k_
+                        vmm = psum.tile([P, 512], F32, name="mm", tag="mm", bufs=3)
+                        mx_pass(vmm[:], tb, l0 + 1, gpos_q[nb], True, True)
+                        if bz == 0:
+                            n_ = work.tile([P, 512], F32, name="nuq", tag="nuq", bufs=2)
+                            nq = n_
+                        else:
+                            n_ = work.tile([P, 512], F32, name="nup", tag="nup", bufs=4)
+                            nup[bx, by] = n_
+                        nc.vector.tensor_tensor(out=n_[:], in0=vmm[:], in1=wt[:], op=ALU.mult)
+                    s_ = work.tile([P, 512], F32, name="nus", tag="nus", bufs=4)
+                    nc.vector.tensor_tensor(out=s_[:], in0=nq[:], in1=nup[bx, by][:], op=ALU.add)
+                    nus[bx, by] = s_
+            return kap, nup, nus
+
+        def add_transposed(out, tiles, j):
+            n = len(tiles)
+            for i, t in enumerate(tiles):
+                nc.tensor.matmul(out, lhsT=t[:, j * P:(j + 1) * P], rhs=ident_f[:],
+                                 start=(i == 0), stop=(i == n - 1), is_transpose=True)
+
+        def sums(kap, nup, nus, j):
+            pairs = [(1, 1), (1, 0), (0, 1), (0, 0)]
+            trip = [(a, c_, d) for a, c_ in pairs for d in (0, 1)]
+            bank_a = psum.tile([P, 4, P], F32, name="sum", tag="sum", bufs=3)
+            add_transposed(bank_a[:, 0, :], [kap[e] for e in trip], j)
+            for i in range(3):
+                add_transposed(bank_a[:, 1 + i, :], [kap[e] for e in trip if e[i] == 1], j)
+            bank_b = psum.tile([P, 4, P], F32, name="sum", tag="sum", bufs=3)
+            add_transposed(bank_b[:, 0, :], [nus[e] for e in pairs], j)
+            for i in range(2):
+                add_transposed(bank_b[:, 1 + i, :], [nus[e] for e in pairs if e[i] == 1], j)
+            add_transposed(bank_b[:, 3, :], [nup[e] for e in pairs], j)
+            return bank_a, bank_b
+
+        def tail(j, bank_a, bank_b, ptok, stok, dz):
+            pt = ptok[j // 2]
+            jj = j % 2
+            m1 = work.tile([P, 4, P], F32, name="m1", tag="tmp", bufs=4)
+            nc.vector.scalar_tensor_tensor(out=m1[:], in0=bank_a[:], scalar=INV_T,
+                                           in1=pt[:, jj, 3:4, :].to_broadcast([P, 4, P]), op0=ALU.mult, op1=ALU.mult)
+            nc.vector.scalar_tensor_tensor(out=dz[:, j, 3, :], in0=bank_a[:, 0, :], scalar=INV_T,
+                                           in1=stok[j // 2][:, jj, :], op0=ALU.mult, op1=ALU.mult)
+            r = work.tile([P, 4, P], F32, name="r", tag="tmp", bufs=4)
+            nc.vector.scalar_tensor_tensor(out=r[:], in0=bank_b[:], scalar=INV_T, in1=m1[:], op0=ALU.mult, op1=ALU.add)
+            m2 = work.tile([P, 3, P], F32, name="m2", tag="tmp", bufs=4)
+            nc.vector.tensor_tensor(out=m2[:], in0=pt[:, jj, 0:3, :], in1=r[:, 0:1, :].to_broadcast([P, 3, P]), op=ALU.mult)
+            nc.vector.tensor_tensor(out=dz[:, j, 0:3, :], in0=r[:, 1:4, :], in1=m2[:], op=ALU.subtract)
+
+        def turn(j, dz, grp):
+            bank = psum.tile([P, DEPTH, P], BF16, name="tr", tag="tr", bufs=2)
+            for lev in range(DEPTH):
+                nc.tensor.transpose(bank[:, lev, :], dz[:, j, lev, :], ident_b[:])
+            nc.scalar.copy(out=grp[:, 512 * j:512 * (j + 1)].rearrange("t (p l) -> t p l", l=DEPTH),
+                           in_=bank[:].rearrange("t l p -> t p l"))
+
+        def finish(tb, nb, dz, grp):
+            quantize(feat_q[tb][nb], slice(0, 512), grp[:], E5)
+            tg = work.tile([P, 2048], BF16, name="grp", tag="grp", bufs=4, align_bytes=64)
+            interleave(tg[:].rearrange("p (c t) -> p c t", t=4), dz[:].rearrange("p j l t -> p j (l t)"))
+            quantize(tok_q[tb][nb], slice(0, 512), tg[:], E5)
+
+        def output_x(nb):
+            for j in range(PACK):
+                acc = psum.tile([P, 512], F32, name="mm", tag="mm", bufs=3)
+                for tb in range(TB):
+                    q = feat_q[tb][nb]
+                    nc.tensor.matmul_mx(out=acc[:], lhsT=q[0][:, j * P:(j + 1) * P].bitcast(E5), lhsT_scale=q[1][:, j * P:(j + 1) * P],
+                                        rhs=w_q[tb][0][:].bitcast(E4), rhs_scale=w_q[tb][1][:], start=(tb == 0), stop=(tb == TB - 1))
+                o = work.tile([P, 512], F32, name="osb", tag="osb", bufs=3)
+                nc.scalar.copy(out=o[:], in_=acc[:])
+                nc.sync.dma_start(out=o0_v[:, nb, j, :], in_=o[:])
+
+        def output_w(tb):
+            for fb in range(4):
+                acc = psum.tile([P, 512], F32, name="mm", tag="mm", bufs=3)
+                for nb in range(NB):
+                    q = tok_q[tb][nb]
+                    nc.tensor.matmul_mx(out=acc[:], lhsT=x_q[nb][0][:, fb * P:(fb + 1) * P].bitcast(E4), lhsT_scale=x_q[nb][1][:, fb * P:(fb + 1) * P],
+                                        rhs=q[0][:].bitcast(E5), rhs_scale=q[1][:], start=(nb == 0), stop=(nb == NB - 1))
+                o = work.tile([P, 512], F32, name="osb", tag="osb", bufs=3)
+                nc.scalar.copy(out=o[:], in_=acc[:])
+                nc.sync.dma_start(out=o1_v[fb * P:(fb + 1) * P, :, tb * P:(tb + 1) * P], in_=o[:].rearrange("f (l t) -> f l t", l=DEPTH))
+
+        chunks = [(tb, nb) for tb in range(TB) for nb in range(NB)]
+        rz = [load_z(*chunks[0])]
+        graw = [load_g(0)]
+        lraw = [load_leaf(0, q) for q in range(4)]
+        state = [prep_p(0, rz[0])]
+        prep_g(0, graw[0])
+        for q in range(4):
+            prep_leaf(0, q, lraw[q], "sv")
+        rz.append(load_z(*chunks[1]))
+        graw.append(load_g(1))
+        wraw, xraw = [], []
+        for c, (tb, nb) in enumerate(chunks):
+            pi, ptok, stok = state[c]
+            kap, nup, nus = stage_one(tb, nb, pi)
+            if c == 0:
+                prep_g(1, graw[1])
+            if c + 1 < len(chunks):
+                state.append(prep_p(c + 1, rz[c + 1]))
+            if c + 2 < len(chunks):
+                rz.append(load_z(*chunks[c + 2]))
+            if c == 0:
+                lraw = [load_leaf(1, q) for q in range(4)]
+                xraw = [load_x(n) for n in range(NB)]
+                for q in range(2):
+                    prep_leaf(1, q, lraw[q], "ss")
+            if c == 1:
+                for q in range(2, 4):
+                    prep_leaf(1, q, lraw[q], "ss")
+                wraw = [load_w(h) for h in range(2)]
+            dz = work.tile([P, PACK, DEPTH, P], BF16, name="dz", tag="dz", bufs=2)
+            grp = work.tile([P, 2048], BF16, name="fgrp", tag="fgrp", bufs=1, align_bytes=64)
+            for j in range(PACK):
+                banks = sums(kap, nup, nus, j)
+                tail(j, banks[0], banks[1], ptok, stok, dz)
+                if j:
+                    turn(j - 1, dz, grp)
+            turn(PACK - 1, dz, grp)
+            finish(tb, nb, dz, grp)
+            if c == 0:
+                for n in range(NB):
+                    prep_x(n, xraw[n])
+            if c == 1:
+                output_w(0)
+                for t in range(TB):
+                    prep_w(t, wraw)
+            if c == 2:
+                output_x(0)
+            if c == 3:
+                output_w(1)
+                output_x(1)

@@ -23,6 +23,7 @@ P = 128
 PACK = 4
 NB = B // (P * PACK)
 TB = T // P
+N = 512
 INV_T = 1.0 / T
 
 
@@ -30,7 +31,7 @@ def tile_neuralobliviousdecisiontree_v_kernel(tc, x, W, b, leaf_values, z, grad_
     nc = tc.nc
     with ExitStack() as ctx:
         const = ctx.enter_context(tc.tile_pool(name="const", bufs=1))
-        raw = ctx.enter_context(tc.tile_pool(name="raw", bufs=8))
+        raw = ctx.enter_context(tc.tile_pool(name="raw", bufs=5))
         work = ctx.enter_context(tc.tile_pool(name="work", bufs=2))
         psum = ctx.enter_context(tc.psum_pool(name="psum", bufs=2))
 
@@ -38,6 +39,7 @@ def tile_neuralobliviousdecisiontree_v_kernel(tc, x, W, b, leaf_values, z, grad_
         make_identity(nc, ident_f[:])
         ident_b = const.tile([P, P], BF16, name="ident_b")
         make_identity(nc, ident_b[:])
+        ctx.enter_context(tc.manual_schedule())
 
         def codes_tile(name, cols):
             c = const.tile([P, cols], U32, name=name + "_c", align_bytes=64)
@@ -45,12 +47,19 @@ def tile_neuralobliviousdecisiontree_v_kernel(tc, x, W, b, leaf_values, z, grad_
             return c, s
 
         leaf_q = [codes_tile("leaf%d" % tb, L * P) for tb in range(TB)]
-        gpos_q = [codes_tile("gpos%d" % nb, 512) for nb in range(NB)]
-        gneg_q = [codes_tile("gneg%d" % nb, 512) for nb in range(NB)]
+        gpos_q = [codes_tile("gpos%d" % nb, N) for nb in range(NB)]
+        gneg_q = [codes_tile("gneg%d" % nb, N) for nb in range(NB)]
         x_q = [codes_tile("x%d" % nb, F) for nb in range(NB)]
         w_q = [codes_tile("w%d" % tb, F) for tb in range(TB)]
-        tok_q = [[codes_tile("tok%d%d" % (tb, nb), 512) for nb in range(NB)] for tb in range(TB)]
-        feat_q = [[codes_tile("feat%d%d" % (tb, nb), 512) for nb in range(NB)] for tb in range(TB)]
+        tok_q = [[codes_tile("tok%d%d" % (tb, nb), N) for nb in range(NB)] for tb in range(TB)]
+        feat_q = [[codes_tile("feat%d%d" % (tb, nb), N) for nb in range(NB)] for tb in range(TB)]
+        kap = const.tile([P, 8, N], F32, name="kap")
+        nup = const.tile([P, 4, N], F32, name="nup")
+        nuq = const.tile([P, 4, N], F32, name="nuq")
+        nus = const.tile([P, 4, N], F32, name="nus")
+        pi = const.tile([P, 8, N], F32, name="pi")
+        alpha = const.tile([P, 4, N], F32, name="alpha")
+        pq = [const.tile([P, 2, N], F32, name="pq%d" % lev) for lev in range(3)]
 
         z_v = z.rearrange("n l t -> (n l) t").rearrange("(g p m) t -> p g m t", p=P, m=PACK * DEPTH)
         g_v = grad_out.rearrange("(g p j) d -> p g j d", p=P, j=PACK)
@@ -58,11 +67,13 @@ def tile_neuralobliviousdecisiontree_v_kernel(tc, x, W, b, leaf_values, z, grad_
         o0_v = out_0.rearrange("(g p j) f -> p g j f", p=P, j=PACK)
         w_v = W.rearrange("l (b p) t -> p b l t", p=P)
         o1_v = out_1.rearrange("l f t -> f l t")
+        chunks = [(tb, nb) for tb in range(TB) for nb in range(NB)]
 
-        def load_z(tb, nb):
+        def load_z(c):
+            tb, nb = chunks[c]
             tiles = []
             for h in range(2):
-                t = raw.tile([P, 2 * DEPTH, P], F32, name="raw", tag="raw")
+                t = raw.tile([P, 2 * DEPTH, P], F32, name="rz", tag="rz", bufs=6)
                 nc.sync.dma_start(out=t[:], in_=z_v[:, nb, 8 * h:8 * h + 8, tb * P:(tb + 1) * P])
                 tiles.append(t)
             return tiles
@@ -88,8 +99,17 @@ def tile_neuralobliviousdecisiontree_v_kernel(tc, x, W, b, leaf_values, z, grad_
                 nc.sync.dma_start(out=t[:, i, :, :], in_=w_v[:, 2 * half + i, :, :])
             return t
 
-        def quantize(q, cols, src, fmt):
-            nc.vector.quantize_mx(out=q[0][:, cols].bitcast(fmt), scales=q[1][:, cols], in_=src)
+        def quantize(q, c0, c1, src, fmt):
+            nc.vector.quantize_mx(out=q[0][:, c0:c1].bitcast(fmt), scales=q[1][:, c0:c1], in_=src)
+
+        def copy_on(eng, dst, src):
+            if eng == "v":
+                nc.vector.tensor_copy(out=dst, in_=src)
+            else:
+                nc.scalar.copy(out=dst, in_=src)
+
+        def grp_tile():
+            return work.tile([P, 2048], BF16, name="grp", tag="grp", bufs=4, align_bytes=64)
 
         def words_bank(src_a, src_b):
             bank = psum.tile([P, 2, 2, P], F32, name="tr", tag="tr", bufs=2)
@@ -99,113 +119,92 @@ def tile_neuralobliviousdecisiontree_v_kernel(tc, x, W, b, leaf_values, z, grad_
                     nc.tensor.transpose(bank[:, i, u, :], words[:, u:256:2], ident_f[:])
             return bank
 
+        def words_out(eng, dst, bank):
+            copy_on(eng, dst.bitcast(F32).rearrange("k (i p u) -> k i p u", i=2, u=2), bank[:].rearrange("k i u p -> k i p u"))
+
         def prep_leaf(tb, q, t, engines):
             for i in range(2):
                 bank = words_bank(t[:, 2 * i, :], t[:, 2 * i + 1, :])
-                grp = work.tile([P, 2 * P * PACK], BF16, name="lgrp", tag="lgrp", bufs=4, align_bytes=64)
-                dst = grp[:].bitcast(F32).rearrange("k (i p u) -> k i p u", i=2, u=2)
-                src = bank[:].rearrange("k i u p -> k i p u")
-                if engines[i] == "v":
-                    nc.vector.tensor_copy(out=dst, in_=src)
-                else:
-                    nc.scalar.copy(out=dst, in_=src)
+                grp = work.tile([P, 1024], BF16, name="lgrp", tag="lgrp", bufs=3, align_bytes=64)
+                words_out(engines[i], grp[:], bank)
                 l0 = 4 * q + 2 * i
-                quantize(leaf_q[tb], slice(l0 * P, (l0 + 2) * P), grp[:], E4)
+                quantize(leaf_q[tb], l0 * P, (l0 + 2) * P, grp[:], E4)
 
-        def prep_g(nb, t):
-            grp = work.tile([P, 2048], BF16, name="grp", tag="grp", bufs=4, align_bytes=64)
+        def prep_g(nb, t, engines):
+            grp = grp_tile()
             for i in range(2):
                 bank = words_bank(t[:, 2 * i, :], t[:, 2 * i + 1, :])
-                dst = grp[:, 1024 * i:1024 * (i + 1)].bitcast(F32).rearrange("k (i p u) -> k i p u", i=2, u=2)
-                nc.scalar.copy(out=dst, in_=bank[:].rearrange("k i u p -> k i p u"))
-            neg = work.tile([P, 2048], BF16, name="grp", tag="grp", bufs=4, align_bytes=64)
+                words_out(engines[i], grp[:, 1024 * i:1024 * (i + 1)], bank)
+            neg = grp_tile()
             nc.vector.tensor_scalar_mul(neg[:], grp[:], -1.0)
-            quantize(gpos_q[nb], slice(0, 512), grp[:], E5)
-            quantize(gneg_q[nb], slice(0, 512), neg[:], E5)
+            quantize(gpos_q[nb], 0, N, grp[:], E5)
+            quantize(gneg_q[nb], 0, N, neg[:], E5)
 
-        def interleave(dst, src):
-            nc.scalar.copy(out=dst.rearrange("p (c i) t -> p c t i", i=4), in_=src.rearrange("p t (c i) -> p c t i", i=4))
+        def interleave(eng, dst, src):
+            copy_on(eng, dst.rearrange("p (c i) t -> p c t i", i=4), src.rearrange("p t (c i) -> p c t i", i=4))
 
         def prep_x(nb, t):
-            grp = work.tile([P, 2048], BF16, name="grp", tag="grp", bufs=4, align_bytes=64)
-            interleave(grp[:].rearrange("p (c t) -> p c t", t=4), t[:])
-            quantize(x_q[nb], slice(0, F), grp[:], E4)
+            grp = grp_tile()
+            interleave("s", grp[:].rearrange("p (c t) -> p c t", t=4), t[:])
+            quantize(x_q[nb], 0, F, grp[:], E4)
 
         def prep_w(tb, halves):
-            grp = work.tile([P, 2048], BF16, name="grp", tag="grp", bufs=4, align_bytes=64)
+            grp = grp_tile()
             for fb in range(4):
                 bank = psum.tile([P, DEPTH, P], BF16, name="tr", tag="tr", bufs=2)
                 for lev in range(DEPTH):
                     nc.tensor.transpose(bank[:, lev, :], halves[fb // 2][:, fb % 2, lev, tb * P:(tb + 1) * P], ident_b[:])
                 nc.scalar.copy(out=grp[:, 512 * fb:512 * (fb + 1)].rearrange("t (f l) -> t f l", l=DEPTH),
                                in_=bank[:].rearrange("t l f -> t f l"))
-            quantize(w_q[tb], slice(0, F), grp[:], E4)
+            quantize(w_q[tb], 0, F, grp[:], E4)
 
-        def prep_p(c, rz):
-            pq = []
-            for lev in range(3):
-                bank = psum.tile([P, 512], F32, name="tr", tag="tr", bufs=2)
-                for j in range(PACK):
-                    nc.tensor.transpose(bank[:, j * P:(j + 1) * P], rz[j // 2][:, (j % 2) * DEPTH + lev, :], ident_f[:])
-                t = work.tile([P, 2, 512], F32, name="pq%d" % lev, tag="pq%d" % lev, bufs=1)
-                nc.scalar.activation(out=t[:, 1, :], in_=bank[:], func=ACT.Sigmoid)
-                nc.scalar.activation(out=t[:, 0, :], in_=bank[:], func=ACT.Sigmoid, scale=-1.0)
-                pq.append(t)
-            ptok, stok = [], []
+        def prep_pq(rz, lev):
+            bank = psum.tile([P, N], F32, name="tr", tag="tr", bufs=2)
+            for j in range(PACK):
+                nc.tensor.transpose(bank[:, j * P:(j + 1) * P], rz[j // 2][:, (j % 2) * DEPTH + lev, :], ident_f[:])
+            nc.scalar.activation(out=pq[lev][:, 1, :], in_=bank[:], func=ACT.Sigmoid)
+            nc.scalar.activation(out=pq[lev][:, 0, :], in_=bank[:], func=ACT.Sigmoid, scale=-1.0)
+
+        def prep_tok(rz):
+            stok = []
             for h in range(2):
-                pt = work.tile([P, 2, DEPTH, P], F32, name="ptok", tag="ptok", bufs=3)
-                nc.scalar.activation(out=pt[:].rearrange("p j l t -> p (j l) t"), in_=rz[h][:], func=ACT.Sigmoid)
                 qw = work.tile([P, 2, P], F32, name="qw", tag="qw", bufs=2)
                 nc.scalar.activation(out=qw[:], in_=rz[h][:, 3:2 * DEPTH:DEPTH, :], func=ACT.Sigmoid, scale=-1.0)
-                st = work.tile([P, 2, P], F32, name="stok", tag="stok", bufs=3)
-                nc.gpsimd.tensor_tensor(out=st[:], in0=pt[:, :, 3, :], in1=qw[:], op=ALU.mult)
-                ptok.append(pt)
+                nc.scalar.activation(out=rz[h][:], in_=rz[h][:], func=ACT.Sigmoid)
+                st = work.tile([P, 2, P], F32, name="stok", tag="stok", bufs=6)
+                nc.gpsimd.tensor_tensor(out=st[:], in0=rz[h][:, 3:2 * DEPTH:DEPTH, :], in1=qw[:], op=ALU.mult)
                 stok.append(st)
-            pi = {}
-            for bx in (1, 0):
-                for by in (1, 0):
-                    al = work.tile([P, 512], F32, name="alpha", tag="alpha", bufs=3)
-                    eng = nc.vector if c == 0 else nc.gpsimd
-                    eng.tensor_tensor(out=al[:], in0=pq[0][:, bx, :], in1=pq[1][:, by, :], op=ALU.mult)
-                    for bz in (0, 1):
-                        w_ = work.tile([P, 512], F32, name="pi", tag="pi", bufs=11)
-                        eng2 = nc.vector if (c == 0 and bz == 0) else nc.gpsimd
-                        eng2.tensor_tensor(out=w_[:], in0=al[:], in1=pq[2][:, bz, :], op=ALU.mult)
-                        pi[bx, by, bz] = w_
-            return pi, ptok, stok
+            return stok
+
+        def make_alpha(eng, a):
+            eng.tensor_tensor(out=alpha[:, a, :], in0=pq[0][:, 1 - a // 2, :], in1=pq[1][:, 1 - a % 2, :], op=ALU.mult)
+
+        def make_pi(eng, i):
+            eng.tensor_tensor(out=pi[:, i, :], in0=alpha[:, i // 2, :], in1=pq[2][:, 1 - i % 2, :], op=ALU.mult)
 
         def mx_pass(out, tb, l, gq, start, stop):
             nc.tensor.matmul_mx(out=out, lhsT=leaf_q[tb][0][:, l * P:(l + 1) * P].bitcast(E4),
                                 lhsT_scale=leaf_q[tb][1][:, l * P:(l + 1) * P],
                                 rhs=gq[0][:].bitcast(E5), rhs_scale=gq[1][:], start=start, stop=stop)
 
-        def stage_one(tb, nb, pi):
-            kap, nup, nus = {}, {}, {}
-            for bx in (1, 0):
-                for by in (1, 0):
-                    nq = None
-                    for bz in (0, 1):
-                        l0 = 8 * (1 - bx) + 4 * (1 - by) + 2 * (1 - bz)
-                        wt = pi[bx, by, bz]
-                        dmm = psum.tile([P, 512], F32, name="mm", tag="mm", bufs=3)
-                        mx_pass(dmm[:], tb, l0, gpos_q[nb], True, False)
-                        mx_pass(dmm[:], tb, l0 + 1, gneg_q[nb], False, True)
-                        k_ = work.tile([P, 512], F32, name="kap", tag="kap", bufs=8)
-                        nc.vector.tensor_tensor(out=k_[:], in0=dmm[:], in1=wt[:], op=ALU.mult)
-                        kap[bx, by, bz] = k_
-                        vmm = psum.tile([P, 512], F32, name="mm", tag="mm", bufs=3)
-                        mx_pass(vmm[:], tb, l0 + 1, gpos_q[nb], True, True)
-                        if bz == 0:
-                            n_ = work.tile([P, 512], F32, name="nuq", tag="nuq", bufs=2)
-                            nq = n_
-                        else:
-                            n_ = work.tile([P, 512], F32, name="nup", tag="nup", bufs=4)
-                            nup[bx, by] = n_
-                        nc.vector.tensor_tensor(out=n_[:], in0=vmm[:], in1=wt[:], op=ALU.mult)
-                    s_ = work.tile([P, 512], F32, name="nus", tag="nus", bufs=4)
-                    nc.vector.tensor_tensor(out=s_[:], in0=nq[:], in1=nup[bx, by][:], op=ALU.add)
-                    nus[bx, by] = s_
-            return kap, nup, nus
+        def mx_group(c, k):
+            tb, nb = chunks[c]
+            i, is_v = k // 2, k % 2
+            mm = psum.tile([P, N], F32, name="mm", tag="mm", bufs=3)
+            if is_v:
+                mx_pass(mm[:], tb, 2 * i + 1, gpos_q[nb], True, True)
+            else:
+                mx_pass(mm[:], tb, 2 * i, gpos_q[nb], True, False)
+                mx_pass(mm[:], tb, 2 * i + 1, gneg_q[nb], False, True)
+            return mm
+
+        def weigh(k, mm):
+            i, is_v = k // 2, k % 2
+            if is_v:
+                dst = nup[:, i // 2, :] if i % 2 == 0 else nuq[:, i // 2, :]
+            else:
+                dst = kap[:, i, :]
+            nc.vector.tensor_tensor(out=dst, in0=mm[:], in1=pi[:, i, :], op=ALU.mult)
 
         def add_transposed(out, tiles, j):
             n = len(tiles)
@@ -213,116 +212,288 @@ def tile_neuralobliviousdecisiontree_v_kernel(tc, x, W, b, leaf_values, z, grad_
                 nc.tensor.matmul(out, lhsT=t[:, j * P:(j + 1) * P], rhs=ident_f[:],
                                  start=(i == 0), stop=(i == n - 1), is_transpose=True)
 
-        def sums(kap, nup, nus, j):
-            pairs = [(1, 1), (1, 0), (0, 1), (0, 0)]
-            trip = [(a, c_, d) for a, c_ in pairs for d in (0, 1)]
-            bank_a = psum.tile([P, 4, P], F32, name="sum", tag="sum", bufs=3)
-            add_transposed(bank_a[:, 0, :], [kap[e] for e in trip], j)
-            for i in range(3):
-                add_transposed(bank_a[:, 1 + i, :], [kap[e] for e in trip if e[i] == 1], j)
-            bank_b = psum.tile([P, 4, P], F32, name="sum", tag="sum", bufs=3)
-            add_transposed(bank_b[:, 0, :], [nus[e] for e in pairs], j)
-            for i in range(2):
-                add_transposed(bank_b[:, 1 + i, :], [nus[e] for e in pairs if e[i] == 1], j)
-            add_transposed(bank_b[:, 3, :], [nup[e] for e in pairs], j)
-            return bank_a, bank_b
+        picks = [[i for i in range(8)], [i for i in range(8) if i < 4], [i for i in range(8) if i % 4 < 2], [i for i in range(8) if i % 2 == 0]]
 
-        def tail(j, bank_a, bank_b, ptok, stok, dz):
-            pt = ptok[j // 2]
-            jj = j % 2
-            m1 = work.tile([P, 4, P], F32, name="m1", tag="tmp", bufs=4)
-            nc.vector.scalar_tensor_tensor(out=m1[:], in0=bank_a[:], scalar=INV_T,
-                                           in1=pt[:, jj, 3:4, :].to_broadcast([P, 4, P]), op0=ALU.mult, op1=ALU.mult)
-            nc.vector.scalar_tensor_tensor(out=dz[:, j, 3, :], in0=bank_a[:, 0, :], scalar=INV_T,
-                                           in1=stok[j // 2][:, jj, :], op0=ALU.mult, op1=ALU.mult)
-            r = work.tile([P, 4, P], F32, name="r", tag="tmp", bufs=4)
-            nc.vector.scalar_tensor_tensor(out=r[:], in0=bank_b[:], scalar=INV_T, in1=m1[:], op0=ALU.mult, op1=ALU.add)
-            m2 = work.tile([P, 3, P], F32, name="m2", tag="tmp", bufs=4)
-            nc.vector.tensor_tensor(out=m2[:], in0=pt[:, jj, 0:3, :], in1=r[:, 0:1, :].to_broadcast([P, 3, P]), op=ALU.mult)
-            nc.vector.tensor_tensor(out=dz[:, j, 0:3, :], in0=r[:, 1:4, :], in1=m2[:], op=ALU.subtract)
+        def sum_a(j):
+            bank = psum.tile([P, 4, P], F32, name="sum", tag="sum", bufs=3)
+            for s in range(4):
+                add_transposed(bank[:, s, :], [kap[:, i, :] for i in picks[s]], j)
+            return bank
 
-        def turn(j, dz, grp):
+        def sum_b(j):
+            bank = psum.tile([P, 4, P], F32, name="sum", tag="sum", bufs=3)
+            add_transposed(bank[:, 3, :], [nup[:, a, :] for a in range(4)], j)
+            for s, sel in enumerate(((0, 1, 2, 3), (0, 1), (0, 2))):
+                add_transposed(bank[:, s, :], [nus[:, a, :] for a in sel], j)
+            return bank
+
+        def tmp_tile(n):
+            return work.tile([P, n, P], F32, name="tmp", tag="tmp", bufs=4)
+
+        def turn(j, dz, grp, eng):
             bank = psum.tile([P, DEPTH, P], BF16, name="tr", tag="tr", bufs=2)
             for lev in range(DEPTH):
                 nc.tensor.transpose(bank[:, lev, :], dz[:, j, lev, :], ident_b[:])
-            nc.scalar.copy(out=grp[:, 512 * j:512 * (j + 1)].rearrange("t (p l) -> t p l", l=DEPTH),
-                           in_=bank[:].rearrange("t l p -> t p l"))
+            copy_on(eng, grp[:, 512 * j:512 * (j + 1)].rearrange("t (p l) -> t p l", l=DEPTH), bank[:].rearrange("t l p -> t p l"))
 
-        def finish(tb, nb, dz, grp):
-            quantize(feat_q[tb][nb], slice(0, 512), grp[:], E5)
-            tg = work.tile([P, 2048], BF16, name="grp", tag="grp", bufs=4, align_bytes=64)
-            interleave(tg[:].rearrange("p (c t) -> p c t", t=4), dz[:].rearrange("p j l t -> p j (l t)"))
-            quantize(tok_q[tb][nb], slice(0, 512), tg[:], E5)
+        def out_x_group(nb, j, eng):
+            acc = psum.tile([P, N], F32, name="sum", tag="sum", bufs=3)
+            for tb in range(TB):
+                q = feat_q[tb][nb]
+                nc.tensor.matmul_mx(out=acc[:], lhsT=q[0][:, j * P:(j + 1) * P].bitcast(E5), lhsT_scale=q[1][:, j * P:(j + 1) * P],
+                                    rhs=w_q[tb][0][:].bitcast(E4), rhs_scale=w_q[tb][1][:], start=(tb == 0), stop=(tb == TB - 1))
+            o = work.tile([P, N], F32, name="osb", tag="osb", bufs=3)
+            copy_on(eng, o[:], acc[:])
+            nc.sync.dma_start(out=o0_v[:, nb, j, :], in_=o[:])
 
-        def output_x(nb):
-            for j in range(PACK):
-                acc = psum.tile([P, 512], F32, name="mm", tag="mm", bufs=3)
-                for tb in range(TB):
-                    q = feat_q[tb][nb]
-                    nc.tensor.matmul_mx(out=acc[:], lhsT=q[0][:, j * P:(j + 1) * P].bitcast(E5), lhsT_scale=q[1][:, j * P:(j + 1) * P],
-                                        rhs=w_q[tb][0][:].bitcast(E4), rhs_scale=w_q[tb][1][:], start=(tb == 0), stop=(tb == TB - 1))
-                o = work.tile([P, 512], F32, name="osb", tag="osb", bufs=3)
-                nc.scalar.copy(out=o[:], in_=acc[:])
-                nc.sync.dma_start(out=o0_v[:, nb, j, :], in_=o[:])
+        def out_w_group(tb, fb, eng):
+            acc = psum.tile([P, N], F32, name="sum", tag="sum", bufs=3)
+            for nb in range(NB):
+                q = tok_q[tb][nb]
+                nc.tensor.matmul_mx(out=acc[:], lhsT=x_q[nb][0][:, fb * P:(fb + 1) * P].bitcast(E4), lhsT_scale=x_q[nb][1][:, fb * P:(fb + 1) * P],
+                                    rhs=q[0][:].bitcast(E5), rhs_scale=q[1][:], start=(nb == 0), stop=(nb == NB - 1))
+            o = work.tile([P, N], F32, name="osb", tag="osb", bufs=3)
+            copy_on(eng, o[:], acc[:])
+            nc.sync.dma_start(out=o1_v[fb * P:(fb + 1) * P, :, tb * P:(tb + 1) * P], in_=o[:].rearrange("f (l t) -> f l t", l=DEPTH))
 
-        def output_w(tb):
-            for fb in range(4):
-                acc = psum.tile([P, 512], F32, name="mm", tag="mm", bufs=3)
-                for nb in range(NB):
-                    q = tok_q[tb][nb]
-                    nc.tensor.matmul_mx(out=acc[:], lhsT=x_q[nb][0][:, fb * P:(fb + 1) * P].bitcast(E4), lhsT_scale=x_q[nb][1][:, fb * P:(fb + 1) * P],
-                                        rhs=q[0][:].bitcast(E5), rhs_scale=q[1][:], start=(nb == 0), stop=(nb == NB - 1))
-                o = work.tile([P, 512], F32, name="osb", tag="osb", bufs=3)
-                nc.scalar.copy(out=o[:], in_=acc[:])
-                nc.sync.dma_start(out=o1_v[fb * P:(fb + 1) * P, :, tb * P:(tb + 1) * P], in_=o[:].rearrange("f (l t) -> f l t", l=DEPTH))
-
-        chunks = [(tb, nb) for tb in range(TB) for nb in range(NB)]
-        rz = [load_z(*chunks[0])]
-        graw = [load_g(0)]
-        lraw = [load_leaf(0, q) for q in range(4)]
-        state = [prep_p(0, rz[0])]
-        prep_g(0, graw[0])
+        rz = [load_z(0)]
+        g_raw = [load_g(0)]
+        leaf_raw = {}
         for q in range(4):
-            prep_leaf(0, q, lraw[q], "sv")
-        rz.append(load_z(*chunks[1]))
-        graw.append(load_g(1))
-        wraw, xraw = [], []
-        for c, (tb, nb) in enumerate(chunks):
-            pi, ptok, stok = state[c]
-            kap, nup, nus = stage_one(tb, nb, pi)
-            if c == 0:
-                prep_g(1, graw[1])
-            if c + 1 < len(chunks):
-                state.append(prep_p(c + 1, rz[c + 1]))
-            if c + 2 < len(chunks):
-                rz.append(load_z(*chunks[c + 2]))
-            if c == 0:
-                lraw = [load_leaf(1, q) for q in range(4)]
-                xraw = [load_x(n) for n in range(NB)]
-                for q in range(2):
-                    prep_leaf(1, q, lraw[q], "ss")
-            if c == 1:
-                for q in range(2, 4):
-                    prep_leaf(1, q, lraw[q], "ss")
-                wraw = [load_w(h) for h in range(2)]
+            leaf_raw[0, q] = load_leaf(0, q)
+        rz.append(load_z(1))
+        g_raw.append(load_g(1))
+        rz.append(load_z(2))
+        for q in range(4):
+            leaf_raw[1, q] = load_leaf(1, q)
+        x_raw = [load_x(nb) for nb in range(NB)]
+        rz.append(load_z(3))
+        w_raw = [load_w(half) for half in range(2)]
+
+        def leaf_turn(tb, q, engines):
+            out = []
+            for i in range(2):
+                bank = words_bank(leaf_raw[tb, q][:, 2 * i, :], leaf_raw[tb, q][:, 2 * i + 1, :])
+                grp = work.tile([P, 1024], BF16, name="lgrp", tag="lgrp", bufs=3, align_bytes=64)
+                words_out(engines[i], grp[:], bank)
+                out.append((tb, 4 * q + 2 * i, grp))
+            return out
+
+        def leaf_quant(items):
+            for tb, l0, grp in items:
+                quantize(leaf_q[tb], l0 * P, (l0 + 2) * P, grp[:], E4)
+
+        def g_turn(nb, engines):
+            grp = grp_tile()
+            for i in range(2):
+                bank = words_bank(g_raw[nb][:, 2 * i, :], g_raw[nb][:, 2 * i + 1, :])
+                words_out(engines[i], grp[:, 1024 * i:1024 * (i + 1)], bank)
+            return grp
+
+        def g_quant(nb, grp):
+            neg = grp_tile()
+            nc.vector.tensor_scalar_mul(neg[:], grp[:], -1.0)
+            quantize(gpos_q[nb], 0, N, grp[:], E5)
+            quantize(gneg_q[nb], 0, N, neg[:], E5)
+
+        def x_turn(nb):
+            grp = grp_tile()
+            interleave("s", grp[:].rearrange("p (c t) -> p c t", t=4), x_raw[nb][:])
+            return grp
+
+        stok = {}
+
+        prep_pq(rz[0], 0)
+        prep_pq(rz[0], 1)
+        g_grp = g_turn(0, "vv")
+        prep_pq(rz[0], 2)
+        for a in range(2):
+            make_alpha(nc.vector, a)
+        g_quant(0, g_grp)
+        for a in range(2, 4):
+            make_alpha(nc.vector, a)
+        groups = []
+        lq = leaf_turn(0, 0, "sv")
+        for a in range(4):
+            make_pi(nc.gpsimd, 2 * a + 1)
+            make_pi(nc.vector, 2 * a)
+            leaf_quant(lq)
+            if a == 0:
+                lq = leaf_turn(0, 1, "ss")
+                stok[0] = prep_tok(rz[0])
+            elif a < 3:
+                lq = leaf_turn(0, a + 1, "ss")
+            if a == 3:
+                prep_pq(rz[1], 0)
+                prep_pq(rz[1], 1)
+                for aa in range(4):
+                    make_alpha(nc.gpsimd, aa)
+                g_grp = g_turn(1, "ss")
+                prep_pq(rz[1], 2)
+            if a >= 1:
+                for k in range(4 * (a - 1), 4 * a):
+                    weigh(k, mx_group(0, k))
+        for k in range(12, 16):
+            weigh(k, mx_group(0, k))
+        for i in range(8):
+            make_pi(nc.gpsimd, i)
+        stok[1] = prep_tok(rz[1])
+        ahead = []
+        x_grp = []
+        tok_grp = {}
+        feat_grp = {}
+
+        def stage_one(c, ahead, extra):
+            banks = list(ahead)
+            for k in range(16):
+                if k + 3 < 16:
+                    pass
+                weigh(k, banks[k])
+                if len(banks) < 16:
+                    banks.append(mx_group(c, len(banks)))
+                if k % 2 == 1 and c + 1 < len(chunks):
+                    make_pi(nc.gpsimd, k // 2)
+                for f in extra.get(k, ()):
+                    f()
+
+        def feat_quant(c):
+            tb, nb = chunks[c]
+            quantize(feat_q[tb][nb], 0, N, feat_grp[c][:], E5)
+
+        def tok_quant(c):
+            tb, nb = chunks[c]
+            quantize(tok_q[tb][nb], 0, N, tok_grp[c][:], E5)
+
+        def tail_phase(c, block, fills, vfills):
+            last = c + 1 == len(chunks)
+            tb, nb = chunks[c]
             dz = work.tile([P, PACK, DEPTH, P], BF16, name="dz", tag="dz", bufs=2)
             grp = work.tile([P, 2048], BF16, name="fgrp", tag="fgrp", bufs=1, align_bytes=64)
-            for j in range(PACK):
-                banks = sums(kap, nup, nus, j)
-                tail(j, banks[0], banks[1], ptok, stok, dz)
-                if j:
-                    turn(j - 1, dz, grp)
-            turn(PACK - 1, dz, grp)
-            finish(tb, nb, dz, grp)
-            if c == 0:
-                for n in range(NB):
-                    prep_x(n, xraw[n])
-            if c == 1:
-                output_w(0)
-                for t in range(TB):
-                    prep_w(t, wraw)
-            if c == 2:
-                output_x(0)
-            if c == 3:
-                output_w(1)
-                output_x(1)
+            feat_grp[c] = grp
+            A, Bk, M1, R, M2 = {}, {}, {}, {}, {}
+
+            def p_tok(j, l0, l1):
+                return rz[c][j // 2][:, (j % 2) * DEPTH + l0:(j % 2) * DEPTH + l1, :]
+
+            def m1(j):
+                M1[j] = tmp_tile(4)
+                nc.vector.scalar_tensor_tensor(out=M1[j][:], in0=A[j][:], scalar=INV_T, in1=p_tok(j, 3, 4).to_broadcast([P, 4, P]),
+                                               op0=ALU.mult, op1=ALU.mult)
+
+            def dzw(j):
+                nc.vector.scalar_tensor_tensor(out=dz[:, j, 3, :], in0=A[j][:, 0, :], scalar=INV_T, in1=stok[c][j // 2][:, j % 2, :],
+                                               op0=ALU.mult, op1=ALU.mult)
+
+            def r(j):
+                R[j] = tmp_tile(4)
+                nc.vector.scalar_tensor_tensor(out=R[j][:], in0=Bk[j][:], scalar=INV_T, in1=M1[j][:], op0=ALU.mult, op1=ALU.add)
+
+            def m2(j):
+                M2[j] = tmp_tile(3)
+                nc.vector.tensor_tensor(out=M2[j][:], in0=p_tok(j, 0, 3), in1=R[j][:, 0:1, :].to_broadcast([P, 3, P]), op=ALU.mult)
+
+            def sub(j):
+                nc.vector.tensor_tensor(out=dz[:, j, 0:3, :], in0=R[j][:, 1:4, :], in1=M2[j][:], op=ALU.subtract)
+
+            def run(fs, i):
+                for f in fs.get(i, ()):
+                    f()
+
+            A[0] = sum_a(0)
+            run(fills, 0)
+            nc.vector.tensor_tensor(out=nus[:], in0=nup[:], in1=nuq[:], op=ALU.add)
+            for f in block:
+                f()
+            Bk[0] = sum_b(0)
+            m1(0)
+            dzw(0)
+            r(0)
+            for j in range(1, 4):
+                A[j] = sum_a(j)
+                run(fills, j)
+                Bk[j] = sum_b(j)
+                m1(j)
+                m2(j - 1)
+                r(j)
+                sub(j - 1)
+                dzw(j)
+                run(vfills, j)
+                if j >= 2:
+                    turn(j - 2, dz, grp, "s")
+                    if last:
+                        quantize(feat_q[tb][nb], (j - 2) * P, (j - 1) * P, grp[:, 512 * (j - 2):512 * (j - 1)], E5)
+            m2(3)
+            run(vfills, 4)
+            sub(3)
+            run(fills, 4)
+            turn(2, dz, grp, "s")
+            ahead = []
+            if not last:
+                ahead = [mx_group(c + 1, k) for k in range(3)]
+            turn(3, dz, grp, "s")
+            tg = grp_tile()
+            tok_grp[c] = tg
+            dst = tg[:].rearrange("p (c t) -> p c t", t=4)
+            src = dz[:].rearrange("p j l t -> p j (l t)")
+            if not last:
+                interleave("s", dst, src)
+            else:
+                interleave("v", dst[:, 0:256, :], src[:, :, 0:256])
+                interleave("s", dst[:, 256:512, :], src[:, :, 256:512])
+                for j in range(2, 4):
+                    quantize(feat_q[tb][nb], j * P, (j + 1) * P, grp[:, 512 * j:512 * (j + 1)], E5)
+                tok_quant(c)
+                for j in range(4):
+                    out_x_group(nb, j, "sv"[j % 2])
+                for fb in range(4):
+                    out_w_group(tb, fb, "sv"[fb % 2])
+            return ahead
+
+        pend = {}
+
+        def later(name, f):
+            def go():
+                pend[name] = f()
+            return go
+
+        def prep_next(c):
+            def alphas():
+                for a in range(4):
+                    make_alpha(nc.gpsimd, a)
+
+            def toks():
+                stok[c + 2] = prep_tok(rz[c + 2])
+            return (lambda: prep_pq(rz[c + 2], 0), lambda: prep_pq(rz[c + 2], 1), alphas, lambda: prep_pq(rz[c + 2], 2), toks)
+
+        n0 = prep_next(0)
+        ahead = tail_phase(0, [lambda: g_quant(1, g_grp)],
+                           {0: [n0[0]], 1: [n0[1], n0[2]], 2: [later("l0", lambda: leaf_turn(1, 0, "ss"))], 3: [n0[3]], 4: [later("l1", lambda: leaf_turn(1, 1, "ss")), n0[4]]},
+                           {3: [lambda: leaf_quant(pend["l0"])]})
+        stage_one(1, ahead, {2: [later("x0", lambda: x_turn(0))], 6: [later("x1", lambda: x_turn(1))]})
+        n1 = prep_next(1)
+        ahead = tail_phase(1, [lambda: leaf_quant(pend["l1"]), lambda: feat_quant(0), lambda: tok_quant(0),
+                               lambda: quantize(x_q[0], 0, F, pend["x0"][:], E4), lambda: quantize(x_q[1], 0, F, pend["x1"][:], E4)],
+                           {0: [n1[0]], 1: [n1[1], n1[2]], 2: [later("l2", lambda: leaf_turn(1, 2, "ss"))], 3: [n1[3]], 4: [later("l3", lambda: leaf_turn(1, 3, "ss")), n1[4]]},
+                           {3: [lambda: leaf_quant(pend["l2"])]})
+        stage_one(2, ahead, {1: [lambda: leaf_quant(pend["l3"])]})
+
+        def w_turn(tb, fb):
+            if fb == 0:
+                pend["w%d" % tb] = grp_tile()
+            grp = pend["w%d" % tb]
+            bank = psum.tile([P, DEPTH, P], BF16, name="tr", tag="tr", bufs=2)
+            for lev in range(DEPTH):
+                nc.tensor.transpose(bank[:, lev, :], w_raw[fb // 2][:, fb % 2, lev, tb * P:(tb + 1) * P], ident_b[:])
+            nc.scalar.copy(out=grp[:, 512 * fb:512 * (fb + 1)].rearrange("t (f l) -> t f l", l=DEPTH), in_=bank[:].rearrange("t l f -> t f l"))
+
+        ahead = tail_phase(2, [lambda: feat_quant(1), lambda: tok_quant(1)],
+                           {0: [lambda: w_turn(0, 0), lambda: w_turn(0, 1)], 1: [lambda: w_turn(0, 2), lambda: w_turn(0, 3)],
+                            2: [lambda: w_turn(1, 0), lambda: w_turn(1, 1)], 3: [lambda: w_turn(1, 2), lambda: w_turn(1, 3)]},
+                           {3: [lambda: quantize(w_q[0], 0, F, pend["w0"][:], E4)]})
+        stage_one(3, ahead, {1: [lambda: quantize(w_q[1], 0, F, pend["w1"][:], E4), lambda: out_w_group(0, 0, "s")],
+                             3: [lambda: feat_quant(2), lambda: out_w_group(0, 1, "s")],
+                             5: [lambda: tok_quant(2), lambda: out_w_group(0, 2, "s")],
+                             7: [lambda: out_w_group(0, 3, "s")],
+                             9: [lambda: out_x_group(0, 0, "s")], 11: [lambda: out_x_group(0, 1, "s")],
+                             13: [lambda: out_x_group(0, 2, "s")], 15: [lambda: out_x_group(0, 3, "s")]})
+        tail_phase(3, [], {}, {})

@@ -190,7 +190,7 @@ def tile_neuralobliviousdecisiontree_v_kernel(tc, x, W, b, leaf_values, z, grad_
         def mx_group(c, k):
             tb, nb = chunks[c]
             i, is_v = k // 2, k % 2
-            mm = psum.tile([P, N], F32, name="mm", tag="mm", bufs=3)
+            mm = psum.tile([P, N], F32, name="big", tag="big", bufs=6)
             if is_v:
                 mx_pass(mm[:], tb, 2 * i + 1, gpos_q[nb], True, True)
             else:
@@ -206,26 +206,27 @@ def tile_neuralobliviousdecisiontree_v_kernel(tc, x, W, b, leaf_values, z, grad_
                 dst = kap[:, i, :]
             nc.vector.tensor_tensor(out=dst, in0=mm[:], in1=pi[:, i, :], op=ALU.mult)
 
-        def add_transposed(out, tiles, j):
-            n = len(tiles)
-            for i, t in enumerate(tiles):
-                nc.tensor.matmul(out, lhsT=t[:, j * P:(j + 1) * P], rhs=ident_f[:],
-                                 start=(i == 0), stop=(i == n - 1), is_transpose=True)
-
         picks = [[i for i in range(8)], [i for i in range(8) if i < 4], [i for i in range(8) if i % 4 < 2], [i for i in range(8) if i % 2 == 0]]
 
-        def sum_a(j):
-            bank = psum.tile([P, 4, P], F32, name="sum", tag="sum", bufs=3)
-            for s in range(4):
-                add_transposed(bank[:, s, :], [kap[:, i, :] for i in picks[s]], j)
-            return bank
+        def steps_a():
+            return [(s, kap, i, n == 0, n + 1 == len(picks[s])) for s in range(4) for n, i in enumerate(picks[s])]
 
-        def sum_b(j):
-            bank = psum.tile([P, 4, P], F32, name="sum", tag="sum", bufs=3)
-            add_transposed(bank[:, 3, :], [nup[:, a, :] for a in range(4)], j)
+        def steps_b():
+            out = [(3, nup, a, a == 0, a == 3) for a in range(4)]
             for s, sel in enumerate(((0, 1, 2, 3), (0, 1), (0, 2))):
-                add_transposed(bank[:, s, :], [nus[:, a, :] for a in sel], j)
-            return bank
+                out.extend([(s, nus, a, n == 0, n + 1 == len(sel)) for n, a in enumerate(sel)])
+            return out
+
+        def sum_pair(steps, j0):
+            banks = []
+            for j in range(2):
+                bank = psum.tile([P, 4, P], F32, name="big", tag="big", bufs=6)
+                banks.append(bank)
+            for s, src, i, first, last in steps:
+                for j in range(2):
+                    nc.tensor.matmul(banks[j][:, s, :], lhsT=src[:, i, (j0 + j) * P:(j0 + j + 1) * P], rhs=ident_f[:],
+                                     start=first, stop=last, is_transpose=True)
+            return banks
 
         def tmp_tile(n):
             return work.tile([P, n, P], F32, name="tmp", tag="tmp", bufs=4)
@@ -237,7 +238,7 @@ def tile_neuralobliviousdecisiontree_v_kernel(tc, x, W, b, leaf_values, z, grad_
             copy_on(eng, grp[:, 512 * j:512 * (j + 1)].rearrange("t (p l) -> t p l", l=DEPTH), bank[:].rearrange("t l p -> t p l"))
 
         def out_x_group(nb, j, eng):
-            acc = psum.tile([P, N], F32, name="sum", tag="sum", bufs=3)
+            acc = psum.tile([P, N], F32, name="big", tag="big", bufs=6)
             for tb in range(TB):
                 q = feat_q[tb][nb]
                 nc.tensor.matmul_mx(out=acc[:], lhsT=q[0][:, j * P:(j + 1) * P].bitcast(E5), lhsT_scale=q[1][:, j * P:(j + 1) * P],
@@ -247,7 +248,7 @@ def tile_neuralobliviousdecisiontree_v_kernel(tc, x, W, b, leaf_values, z, grad_
             nc.sync.dma_start(out=o0_v[:, nb, j, :], in_=o[:])
 
         def out_w_group(tb, fb, eng):
-            acc = psum.tile([P, N], F32, name="sum", tag="sum", bufs=3)
+            acc = psum.tile([P, N], F32, name="big", tag="big", bufs=6)
             for nb in range(NB):
                 q = tok_q[tb][nb]
                 nc.tensor.matmul_mx(out=acc[:], lhsT=x_q[nb][0][:, fb * P:(fb + 1) * P].bitcast(E4), lhsT_scale=x_q[nb][1][:, fb * P:(fb + 1) * P],
@@ -399,37 +400,36 @@ def tile_neuralobliviousdecisiontree_v_kernel(tc, x, W, b, leaf_values, z, grad_
                 for f in fs.get(i, ()):
                     f()
 
-            A[0] = sum_a(0)
+            A[0], A[1] = sum_pair(steps_a(), 0)
             run(fills, 0)
             nc.vector.tensor_tensor(out=nus[:], in0=nup[:], in1=nuq[:], op=ALU.add)
             for f in block:
                 f()
-            Bk[0] = sum_b(0)
-            m1(0)
-            dzw(0)
-            r(0)
-            for j in range(1, 4):
-                A[j] = sum_a(j)
-                run(fills, j)
-                Bk[j] = sum_b(j)
-                m1(j)
-                m2(j - 1)
-                r(j)
-                sub(j - 1)
-                dzw(j)
-                run(vfills, j)
-                if j >= 2:
-                    turn(j - 2, dz, grp, "s")
-                    if last:
-                        quantize(feat_q[tb][nb], (j - 2) * P, (j - 1) * P, grp[:, 512 * (j - 2):512 * (j - 1)], E5)
-            m2(3)
-            run(vfills, 4)
-            sub(3)
+            Bk[0], Bk[1] = sum_pair(steps_b(), 0)
+            for f in (m1, dzw, r):
+                f(0)
+                f(1)
+            A[2], A[3] = sum_pair(steps_a(), 2)
+            run(fills, 1)
+            for f in (m2, sub):
+                f(0)
+                f(1)
+            Bk[2], Bk[3] = sum_pair(steps_b(), 2)
+            run(fills, 2)
+            run(vfills, 3)
+            for f in (m1, dzw, r, m2, sub):
+                f(2)
+                f(3)
+            for j in range(2):
+                turn(j, dz, grp, "s")
+                if last:
+                    quantize(feat_q[tb][nb], j * P, (j + 1) * P, grp[:, 512 * j:512 * (j + 1)], E5)
+            run(fills, 3)
             run(fills, 4)
-            turn(2, dz, grp, "s")
             ahead = []
             if not last:
                 ahead = [mx_group(c + 1, k) for k in range(3)]
+            turn(2, dz, grp, "s")
             turn(3, dz, grp, "s")
             tg = grp_tile()
             tok_grp[c] = tg

@@ -21,9 +21,12 @@ ACT = mybir.ActivationFunctionType
 
 P = 128
 PACK = 4
-NB = B // (P * PACK)
+N = P * PACK
+NB = B // N
 TB = T // P
-N = 512
+PAIRS = L // 2
+AHEAD = 3
+SUMMED = 3
 INV_T = 1.0 / T
 
 
@@ -39,27 +42,29 @@ def tile_neuralobliviousdecisiontree_v_kernel(tc, x, W, b, leaf_values, z, grad_
         make_identity(nc, ident_f[:])
         ident_b = const.tile([P, P], BF16, name="ident_b")
         make_identity(nc, ident_b[:])
+
         ctx.enter_context(tc.manual_schedule())
 
-        def codes_tile(name, cols):
-            c = const.tile([P, cols], U32, name=name + "_c", align_bytes=64)
-            s = const.tile([P, cols], U8, name=name + "_s", align_bytes=64)
-            return c, s
+        def codes_and_scales(name, cols):
+            codes = const.tile([P, cols], U32, name=name + "_c", align_bytes=64)
+            scales = const.tile([P, cols], U8, name=name + "_s", align_bytes=64)
+            return codes, scales
 
-        leaf_q = [codes_tile("leaf%d" % tb, L * P) for tb in range(TB)]
-        gpos_q = [codes_tile("gpos%d" % nb, N) for nb in range(NB)]
-        gneg_q = [codes_tile("gneg%d" % nb, N) for nb in range(NB)]
-        x_q = [codes_tile("x%d" % nb, F) for nb in range(NB)]
-        w_q = [codes_tile("w%d" % tb, F) for tb in range(TB)]
-        tok_q = [[codes_tile("tok%d%d" % (tb, nb), N) for nb in range(NB)] for tb in range(TB)]
-        feat_q = [[codes_tile("feat%d%d" % (tb, nb), N) for nb in range(NB)] for tb in range(TB)]
-        kap = const.tile([P, 8, N], F32, name="kap")
-        nup = const.tile([P, 4, N], F32, name="nup")
-        nuq = const.tile([P, 4, N], F32, name="nuq")
-        nus = const.tile([P, 4, N], F32, name="nus")
-        pi = const.tile([P, 8, N], F32, name="pi")
-        alpha = const.tile([P, 4, N], F32, name="alpha")
-        pq = [const.tile([P, 2, N], F32, name="pq%d" % lev) for lev in range(3)]
+        leaf_q = [codes_and_scales("leaf%d" % tb, L * P) for tb in range(TB)]
+        gpos_q = [codes_and_scales("gpos%d" % nb, N) for nb in range(NB)]
+        gneg_q = [codes_and_scales("gneg%d" % nb, N) for nb in range(NB)]
+        x_q = [codes_and_scales("x%d" % nb, F) for nb in range(NB)]
+        w_q = [codes_and_scales("w%d" % tb, F) for tb in range(TB)]
+        tok_q = [[codes_and_scales("tok%d%d" % (tb, nb), N) for nb in range(NB)] for tb in range(TB)]
+        feat_q = [[codes_and_scales("feat%d%d" % (tb, nb), N) for nb in range(NB)] for tb in range(TB)]
+        rise = const.tile([P, PAIRS, N], F32, name="rise")
+        base_p = const.tile([P, 4, N], F32, name="base_p")
+        base_q = const.tile([P, 4, N], F32, name="base_q")
+        base_sum = const.tile([P, SUMMED, N], F32, name="base_sum")
+        weight01 = const.tile([P, 4, N], F32, name="weight01")
+        gates = [const.tile([P, 2, N], F32, name="gates%d" % lev) for lev in range(3)]
+        weights = {}
+        qtok = {}
 
         z_v = z.rearrange("n l t -> (n l) t").rearrange("(g p m) t -> p g m t", p=P, m=PACK * DEPTH)
         g_v = grad_out.rearrange("(g p j) d -> p g j d", p=P, j=PACK)
@@ -68,29 +73,25 @@ def tile_neuralobliviousdecisiontree_v_kernel(tc, x, W, b, leaf_values, z, grad_
         w_v = W.rearrange("l (b p) t -> p b l t", p=P)
         o1_v = out_1.rearrange("l f t -> f l t")
         chunks = [(tb, nb) for tb in range(TB) for nb in range(NB)]
+        last_chunk = len(chunks) - 1
 
         def load_z(c):
             tb, nb = chunks[c]
             tiles = []
             for h in range(2):
-                t = raw.tile([P, 2 * DEPTH, P], F32, name="rz", tag="rz", bufs=6)
+                t = raw.tile([P, 2 * DEPTH, P], F32, name="ztile", tag="ztile", bufs=6)
                 nc.sync.dma_start(out=t[:], in_=z_v[:, nb, 8 * h:8 * h + 8, tb * P:(tb + 1) * P])
                 tiles.append(t)
             return tiles
 
-        def load_g(nb):
-            t = raw.tile([P, PACK, DO], BF16, name="raw", tag="raw")
-            nc.sync.dma_start(out=t[:], in_=g_v[:, nb, :, :])
+        def load_tokens(view, nb):
+            t = raw.tile([P, PACK, 512], BF16, name="raw", tag="raw")
+            nc.sync.dma_start(out=t[:], in_=view[:, nb, :, :])
             return t
 
-        def load_leaf(tb, q):
+        def load_leaves(tb, part):
             t = raw.tile([P, 4, DO], BF16, name="raw", tag="raw")
-            nc.sync.dma_start(out=t[:], in_=leaf_values[tb * P:(tb + 1) * P, 4 * q:4 * q + 4, :])
-            return t
-
-        def load_x(nb):
-            t = raw.tile([P, PACK, F], BF16, name="raw", tag="raw")
-            nc.sync.dma_start(out=t[:], in_=x_v[:, nb, :, :])
+            nc.sync.dma_start(out=t[:], in_=leaf_values[tb * P:(tb + 1) * P, 4 * part:4 * part + 4, :])
             return t
 
         def load_w(half):
@@ -98,6 +99,20 @@ def tile_neuralobliviousdecisiontree_v_kernel(tc, x, W, b, leaf_values, z, grad_
             for i in range(2):
                 nc.sync.dma_start(out=t[:, i, :, :], in_=w_v[:, 2 * half + i, :, :])
             return t
+
+        g_raw = [load_tokens(g_v, 0)]
+        z_raw = [load_z(0)]
+        leaf_raw = {}
+        for part in range(4):
+            leaf_raw[0, part] = load_leaves(0, part)
+        z_raw.append(load_z(1))
+        g_raw.append(load_tokens(g_v, 1))
+        z_raw.append(load_z(2))
+        for part in range(4):
+            leaf_raw[1, part] = load_leaves(1, part)
+        x_raw = [load_tokens(x_v, nb) for nb in range(NB)]
+        z_raw.append(load_z(3))
+        w_raw = [load_w(half) for half in range(2)]
 
         def quantize(q, c0, c1, src, fmt):
             nc.vector.quantize_mx(out=q[0][:, c0:c1].bitcast(fmt), scales=q[1][:, c0:c1], in_=src)
@@ -108,392 +123,397 @@ def tile_neuralobliviousdecisiontree_v_kernel(tc, x, W, b, leaf_values, z, grad_
             else:
                 nc.scalar.copy(out=dst, in_=src)
 
-        def grp_tile():
-            return work.tile([P, 2048], BF16, name="grp", tag="grp", bufs=4, align_bytes=64)
+        def group_tile():
+            return work.tile([P, PACK * 512], BF16, name="grp", tag="grp", bufs=4, align_bytes=64)
 
-        def words_bank(src_a, src_b):
-            bank = psum.tile([P, 2, 2, P], F32, name="tr", tag="tr", bufs=2)
-            for i, s in enumerate((src_a, src_b)):
-                words = s.bitcast(F32)
+        def bank_tile():
+            return psum.tile([P, N], F32, name="bank", tag="bank", bufs=6)
+
+        def turn_rows(dst, rows_a, rows_b, eng):
+            bank = psum.tile([P, 2, 2, P], F32, name="turned", tag="turned", bufs=2)
+            for i, rows in enumerate((rows_a, rows_b)):
+                words = rows.bitcast(F32)
                 for u in range(2):
                     nc.tensor.transpose(bank[:, i, u, :], words[:, u:256:2], ident_f[:])
-            return bank
+            copy_on(eng, dst.bitcast(F32).rearrange("k (i r u) -> k i r u", i=2, u=2), bank[:].rearrange("k i u r -> k i r u"))
 
-        def words_out(eng, dst, bank):
-            copy_on(eng, dst.bitcast(F32).rearrange("k (i p u) -> k i p u", i=2, u=2), bank[:].rearrange("k i u p -> k i p u"))
-
-        def prep_leaf(tb, q, t, engines):
-            for i in range(2):
-                bank = words_bank(t[:, 2 * i, :], t[:, 2 * i + 1, :])
-                grp = work.tile([P, 1024], BF16, name="lgrp", tag="lgrp", bufs=3, align_bytes=64)
-                words_out(engines[i], grp[:], bank)
-                l0 = 4 * q + 2 * i
-                quantize(leaf_q[tb], l0 * P, (l0 + 2) * P, grp[:], E4)
-
-        def prep_g(nb, t, engines):
-            grp = grp_tile()
-            for i in range(2):
-                bank = words_bank(t[:, 2 * i, :], t[:, 2 * i + 1, :])
-                words_out(engines[i], grp[:, 1024 * i:1024 * (i + 1)], bank)
-            neg = grp_tile()
-            nc.vector.tensor_scalar_mul(neg[:], grp[:], -1.0)
-            quantize(gpos_q[nb], 0, N, grp[:], E5)
-            quantize(gneg_q[nb], 0, N, neg[:], E5)
-
-        def interleave(eng, dst, src):
-            copy_on(eng, dst.rearrange("p (c i) t -> p c t i", i=4), src.rearrange("p t (c i) -> p c t i", i=4))
-
-        def prep_x(nb, t):
-            grp = grp_tile()
-            interleave("s", grp[:].rearrange("p (c t) -> p c t", t=4), t[:])
-            quantize(x_q[nb], 0, F, grp[:], E4)
-
-        def prep_w(tb, halves):
-            grp = grp_tile()
-            for fb in range(4):
-                bank = psum.tile([P, DEPTH, P], BF16, name="tr", tag="tr", bufs=2)
-                for lev in range(DEPTH):
-                    nc.tensor.transpose(bank[:, lev, :], halves[fb // 2][:, fb % 2, lev, tb * P:(tb + 1) * P], ident_b[:])
-                nc.scalar.copy(out=grp[:, 512 * fb:512 * (fb + 1)].rearrange("t (f l) -> t f l", l=DEPTH),
-                               in_=bank[:].rearrange("t l f -> t f l"))
-            quantize(w_q[tb], 0, F, grp[:], E4)
-
-        def prep_pq(rz, lev):
-            bank = psum.tile([P, N], F32, name="tr", tag="tr", bufs=2)
-            for j in range(PACK):
-                nc.tensor.transpose(bank[:, j * P:(j + 1) * P], rz[j // 2][:, (j % 2) * DEPTH + lev, :], ident_f[:])
-            nc.scalar.activation(out=pq[lev][:, 1, :], in_=bank[:], func=ACT.Sigmoid)
-            nc.scalar.activation(out=pq[lev][:, 0, :], in_=bank[:], func=ACT.Sigmoid, scale=-1.0)
-
-        def prep_tok(rz):
-            stok = []
-            for h in range(2):
-                qw = work.tile([P, 2, P], F32, name="qw", tag="qw", bufs=2)
-                nc.scalar.activation(out=qw[:], in_=rz[h][:, 3:2 * DEPTH:DEPTH, :], func=ACT.Sigmoid, scale=-1.0)
-                nc.scalar.activation(out=rz[h][:], in_=rz[h][:], func=ACT.Sigmoid)
-                st = work.tile([P, 2, P], F32, name="stok", tag="stok", bufs=6)
-                nc.gpsimd.tensor_tensor(out=st[:], in0=rz[h][:, 3:2 * DEPTH:DEPTH, :], in1=qw[:], op=ALU.mult)
-                stok.append(st)
-            return stok
-
-        def make_alpha(eng, a):
-            eng.tensor_tensor(out=alpha[:, a, :], in0=pq[0][:, 1 - a // 2, :], in1=pq[1][:, 1 - a % 2, :], op=ALU.mult)
-
-        def make_pi(eng, i):
-            eng.tensor_tensor(out=pi[:, i, :], in0=alpha[:, i // 2, :], in1=pq[2][:, 1 - i % 2, :], op=ALU.mult)
-
-        def mx_pass(out, tb, l, gq, start, stop):
-            nc.tensor.matmul_mx(out=out, lhsT=leaf_q[tb][0][:, l * P:(l + 1) * P].bitcast(E4),
-                                lhsT_scale=leaf_q[tb][1][:, l * P:(l + 1) * P],
-                                rhs=gq[0][:].bitcast(E5), rhs_scale=gq[1][:], start=start, stop=stop)
-
-        def mx_group(c, k):
-            tb, nb = chunks[c]
-            i, is_v = k // 2, k % 2
-            mm = psum.tile([P, N], F32, name="big", tag="big", bufs=6)
-            if is_v:
-                mx_pass(mm[:], tb, 2 * i + 1, gpos_q[nb], True, True)
-            else:
-                mx_pass(mm[:], tb, 2 * i, gpos_q[nb], True, False)
-                mx_pass(mm[:], tb, 2 * i + 1, gneg_q[nb], False, True)
-            return mm
-
-        def weigh(k, mm):
-            i, is_v = k // 2, k % 2
-            if is_v:
-                dst = nup[:, i // 2, :] if i % 2 == 0 else nuq[:, i // 2, :]
-            else:
-                dst = kap[:, i, :]
-            nc.vector.tensor_tensor(out=dst, in0=mm[:], in1=pi[:, i, :], op=ALU.mult)
-
-        picks = [[i for i in range(8)], [i for i in range(8) if i < 4], [i for i in range(8) if i % 4 < 2], [i for i in range(8) if i % 2 == 0]]
-
-        def steps_a():
-            return [(s, kap, i, n == 0, n + 1 == len(picks[s])) for s in range(4) for n, i in enumerate(picks[s])]
-
-        def steps_b():
-            out = [(3, nup, a, a == 0, a == 3) for a in range(4)]
-            for s, sel in enumerate(((0, 1, 2, 3), (0, 1), (0, 2))):
-                out.extend([(s, nus, a, n == 0, n + 1 == len(sel)) for n, a in enumerate(sel)])
-            return out
-
-        def sum_pair(steps, j0):
-            banks = []
-            for j in range(2):
-                bank = psum.tile([P, 4, P], F32, name="big", tag="big", bufs=6)
-                banks.append(bank)
-            for s, src, i, first, last in steps:
-                for j in range(2):
-                    nc.tensor.matmul(banks[j][:, s, :], lhsT=src[:, i, (j0 + j) * P:(j0 + j + 1) * P], rhs=ident_f[:],
-                                     start=first, stop=last, is_transpose=True)
-            return banks
-
-        def tmp_tile(n):
-            return work.tile([P, n, P], F32, name="tmp", tag="tmp", bufs=4)
-
-        def turn(j, dz, grp, eng):
-            bank = psum.tile([P, DEPTH, P], BF16, name="tr", tag="tr", bufs=2)
-            for lev in range(DEPTH):
-                nc.tensor.transpose(bank[:, lev, :], dz[:, j, lev, :], ident_b[:])
-            copy_on(eng, grp[:, 512 * j:512 * (j + 1)].rearrange("t (p l) -> t p l", l=DEPTH), bank[:].rearrange("t l p -> t p l"))
-
-        def out_x_group(nb, j, eng):
-            acc = psum.tile([P, N], F32, name="big", tag="big", bufs=6)
-            for tb in range(TB):
-                q = feat_q[tb][nb]
-                nc.tensor.matmul_mx(out=acc[:], lhsT=q[0][:, j * P:(j + 1) * P].bitcast(E5), lhsT_scale=q[1][:, j * P:(j + 1) * P],
-                                    rhs=w_q[tb][0][:].bitcast(E4), rhs_scale=w_q[tb][1][:], start=(tb == 0), stop=(tb == TB - 1))
-            o = work.tile([P, N], F32, name="osb", tag="osb", bufs=3)
-            copy_on(eng, o[:], acc[:])
-            nc.sync.dma_start(out=o0_v[:, nb, j, :], in_=o[:])
-
-        def out_w_group(tb, fb, eng):
-            acc = psum.tile([P, N], F32, name="big", tag="big", bufs=6)
-            for nb in range(NB):
-                q = tok_q[tb][nb]
-                nc.tensor.matmul_mx(out=acc[:], lhsT=x_q[nb][0][:, fb * P:(fb + 1) * P].bitcast(E4), lhsT_scale=x_q[nb][1][:, fb * P:(fb + 1) * P],
-                                    rhs=q[0][:].bitcast(E5), rhs_scale=q[1][:], start=(nb == 0), stop=(nb == NB - 1))
-            o = work.tile([P, N], F32, name="osb", tag="osb", bufs=3)
-            copy_on(eng, o[:], acc[:])
-            nc.sync.dma_start(out=o1_v[fb * P:(fb + 1) * P, :, tb * P:(tb + 1) * P], in_=o[:].rearrange("f (l t) -> f l t", l=DEPTH))
-
-        rz = [load_z(0)]
-        g_raw = [load_g(0)]
-        leaf_raw = {}
-        for q in range(4):
-            leaf_raw[0, q] = load_leaf(0, q)
-        rz.append(load_z(1))
-        g_raw.append(load_g(1))
-        rz.append(load_z(2))
-        for q in range(4):
-            leaf_raw[1, q] = load_leaf(1, q)
-        x_raw = [load_x(nb) for nb in range(NB)]
-        rz.append(load_z(3))
-        w_raw = [load_w(half) for half in range(2)]
-
-        def leaf_turn(tb, q, engines):
+        def leaf_turn(tb, part):
             out = []
             for i in range(2):
-                bank = words_bank(leaf_raw[tb, q][:, 2 * i, :], leaf_raw[tb, q][:, 2 * i + 1, :])
-                grp = work.tile([P, 1024], BF16, name="lgrp", tag="lgrp", bufs=3, align_bytes=64)
-                words_out(engines[i], grp[:], bank)
-                out.append((tb, 4 * q + 2 * i, grp))
+                grp = work.tile([P, 2 * P * PACK], BF16, name="lgrp", tag="lgrp", bufs=4, align_bytes=64)
+                t = leaf_raw[tb, part]
+                turn_rows(grp[:], t[:, 2 * i, :], t[:, 2 * i + 1, :], "s")
+                out.append((tb, 4 * part + 2 * i, grp))
             return out
 
-        def leaf_quant(items):
-            for tb, l0, grp in items:
-                quantize(leaf_q[tb], l0 * P, (l0 + 2) * P, grp[:], E4)
+        def leaf_quantize(items):
+            for tb, leaf, grp in items:
+                quantize(leaf_q[tb], leaf * P, (leaf + 2) * P, grp[:], E4)
 
         def g_turn(nb, engines):
-            grp = grp_tile()
+            grp = group_tile()
             for i in range(2):
-                bank = words_bank(g_raw[nb][:, 2 * i, :], g_raw[nb][:, 2 * i + 1, :])
-                words_out(engines[i], grp[:, 1024 * i:1024 * (i + 1)], bank)
+                turn_rows(grp[:, 1024 * i:1024 * (i + 1)], g_raw[nb][:, 2 * i, :], g_raw[nb][:, 2 * i + 1, :], engines[i])
             return grp
 
-        def g_quant(nb, grp):
-            neg = grp_tile()
+        def g_quantize(nb, grp):
+            neg = group_tile()
             nc.vector.tensor_scalar_mul(neg[:], grp[:], -1.0)
             quantize(gpos_q[nb], 0, N, grp[:], E5)
             quantize(gneg_q[nb], 0, N, neg[:], E5)
 
+        def interleave(eng, grp, src):
+            dst = grp[:].rearrange("p (c i j) -> p c j i", i=4, j=PACK)
+            copy_on(eng, dst, src.rearrange("p j (c i) -> p c j i", i=4))
+
         def x_turn(nb):
-            grp = grp_tile()
-            interleave("s", grp[:].rearrange("p (c t) -> p c t", t=4), x_raw[nb][:])
+            grp = group_tile()
+            interleave("s", grp, x_raw[nb][:])
             return grp
 
-        stok = {}
+        def w_turn(tb, fb, grp):
+            bank = psum.tile([P, DEPTH, P], BF16, name="turned", tag="turned", bufs=2)
+            for lev in range(DEPTH):
+                nc.tensor.transpose(bank[:, lev, :], w_raw[fb // 2][:, fb % 2, lev, tb * P:(tb + 1) * P], ident_b[:])
+            nc.scalar.copy(out=grp[:, N * fb:N * (fb + 1)].rearrange("t (f l) -> t f l", l=DEPTH), in_=bank[:].rearrange("t l f -> t f l"))
 
-        prep_pq(rz[0], 0)
-        prep_pq(rz[0], 1)
-        g_grp = g_turn(0, "vv")
-        prep_pq(rz[0], 2)
-        for a in range(2):
-            make_alpha(nc.vector, a)
-        g_quant(0, g_grp)
-        for a in range(2, 4):
-            make_alpha(nc.vector, a)
-        groups = []
-        lq = leaf_turn(0, 0, "sv")
-        for a in range(4):
-            make_pi(nc.gpsimd, 2 * a + 1)
-            make_pi(nc.vector, 2 * a)
-            leaf_quant(lq)
-            if a == 0:
-                lq = leaf_turn(0, 1, "ss")
-                stok[0] = prep_tok(rz[0])
-            elif a < 3:
-                lq = leaf_turn(0, a + 1, "ss")
-            if a == 3:
-                prep_pq(rz[1], 0)
-                prep_pq(rz[1], 1)
-                for aa in range(4):
-                    make_alpha(nc.gpsimd, aa)
-                g_grp = g_turn(1, "ss")
-                prep_pq(rz[1], 2)
-            if a >= 1:
-                for k in range(4 * (a - 1), 4 * a):
-                    weigh(k, mx_group(0, k))
-        for k in range(12, 16):
-            weigh(k, mx_group(0, k))
-        for i in range(8):
-            make_pi(nc.gpsimd, i)
-        stok[1] = prep_tok(rz[1])
-        ahead = []
-        x_grp = []
+        def z_turn(c, lev, bank):
+            for j in range(PACK):
+                nc.tensor.transpose(bank[:, j * P:(j + 1) * P], z_raw[c][j // 2][:, (j % 2) * DEPTH + lev, :], ident_f[:])
+
+        def gate(lev, which, bank):
+            nc.scalar.activation(out=gates[lev][:, which, :], in_=bank[:], func=ACT.Sigmoid, scale=-1.0 if which else 1.0)
+
+        def make_gates(c, lev):
+            bank = psum.tile([P, N], F32, name="turned", tag="turned", bufs=2)
+            z_turn(c, lev, bank)
+            gate(lev, 0, bank)
+            gate(lev, 1, bank)
+
+        def make_token_gates(c):
+            qtok[c] = []
+            for h in range(2):
+                t = work.tile([P, 2, P], F32, name="qtok", tag="qtok", bufs=4)
+                nc.scalar.activation(out=t[:], in_=z_raw[c][h][:, 3:2 * DEPTH:DEPTH, :], func=ACT.Sigmoid, scale=-1.0)
+                nc.scalar.activation(out=z_raw[c][h][:], in_=z_raw[c][h][:], func=ACT.Sigmoid)
+                qtok[c].append(t)
+
+        def make_weight01():
+            for i in range(2):
+                nc.vector.tensor_tensor(out=weight01[:, 2 * i:2 * i + 2, :], in0=gates[0][:, i:i + 1, :].to_broadcast([P, 2, N]),
+                                        in1=gates[1][:], op=ALU.mult)
+
+        def weight_tile(c, a):
+            weights[c, a] = work.tile([P, 2, N], F32, name="weight", tag="weight", bufs=7)
+            return weights[c, a]
+
+        def make_weights(c, a):
+            t = weight_tile(c, a)
+            nc.gpsimd.tensor_tensor(out=t[:], in0=weight01[:, a:a + 1, :].to_broadcast([P, 2, N]), in1=gates[2][:], op=ALU.mult)
+
+        def make_first_weights(eng, a):
+            eng.tensor_tensor(out=weight01[:, a, :], in0=gates[0][:, a // 2, :], in1=gates[1][:, a % 2, :], op=ALU.mult)
+            t = weight_tile(0, a)
+            for i in range(2):
+                eng.tensor_tensor(out=t[:, i, :], in0=weight01[:, a, :], in1=gates[2][:, i, :], op=ALU.mult)
+
+        def leaf_pass(bank, tb, leaf, q, start, stop):
+            nc.tensor.matmul_mx(out=bank[:], lhsT=leaf_q[tb][0][:, leaf * P:(leaf + 1) * P].bitcast(E4),
+                                lhsT_scale=leaf_q[tb][1][:, leaf * P:(leaf + 1) * P],
+                                rhs=q[0][:].bitcast(E5), rhs_scale=q[1][:], start=start, stop=stop)
+
+        def leaf_group(c, k):
+            tb, nb = chunks[c]
+            bank = bank_tile()
+            if k % 2:
+                leaf_pass(bank, tb, k, gpos_q[nb], True, True)
+            else:
+                leaf_pass(bank, tb, k, gpos_q[nb], True, False)
+                leaf_pass(bank, tb, k + 1, gneg_q[nb], False, True)
+            return bank
+
+        def weigh(c, k, bank):
+            a, odd = k // 4, (k // 2) % 2
+            if k % 2 == 0:
+                dst = rise[:, k // 2, :]
+            else:
+                dst = base_q[:, a, :] if odd else base_p[:, a, :]
+            nc.vector.tensor_tensor(out=dst, in0=bank[:], in1=weights[c, a][:, odd, :], op=ALU.mult)
+
+        def weigh_chunk(c, banks, extras):
+            for k in range(2 * PAIRS):
+                if k % 4 == 0 and c < last_chunk:
+                    make_weights(c + 1, k // 4)
+                weigh(c, k, banks[k])
+                if len(banks) < 2 * PAIRS:
+                    banks.append(leaf_group(c, len(banks)))
+                for f in extras.get(k, ()):
+                    f()
+
+        rise_terms = []
+        for s, chosen in enumerate((range(8), range(4), (0, 1, 4, 5), (0, 2, 4, 6))):
+            rise_terms.append((s, [(rise, i) for i in chosen]))
+        base_terms = [(3, [(base_p, a) for a in range(4)])]
+        for s, chosen in enumerate((range(4), (0, 1), (0, 2))):
+            terms = []
+            for a in chosen:
+                terms.extend([(base_sum, a)] if a < SUMMED else [(base_p, a), (base_q, a)])
+            base_terms.append((s, terms))
+
+        def turned_sums(sums, j0):
+            banks = []
+            for j in range(2):
+                bank = psum.tile([P, 4, P], F32, name="bank", tag="bank", bufs=6)
+                banks.append(bank)
+            for s, terms in sums:
+                for n, (src, i) in enumerate(terms):
+                    for j in range(2):
+                        nc.tensor.matmul(banks[j][:, s, :], lhsT=src[:, i, (j0 + j) * P:(j0 + j + 1) * P], rhs=ident_f[:],
+                                         start=(n == 0), stop=(n + 1 == len(terms)), is_transpose=True)
+            return banks
+
+        def turn_dz(dz, grp, j):
+            bank = psum.tile([P, DEPTH, P], BF16, name="turned", tag="turned", bufs=2)
+            for lev in range(DEPTH):
+                nc.tensor.transpose(bank[:, lev, :], dz[:, j, lev, :], ident_b[:])
+            nc.scalar.copy(out=grp[:, N * j:N * (j + 1)].rearrange("t (p l) -> t p l", l=DEPTH), in_=bank[:].rearrange("t l p -> t p l"))
+
+        def stage_tile():
+            return raw.tile([P, 2, N], F32, name="ztile", tag="ztile", bufs=6)
+
+        def x_pass(bank, nb, j, tb):
+            q = feat_q[tb][nb]
+            nc.tensor.matmul_mx(out=bank[:], lhsT=q[0][:, j * P:(j + 1) * P].bitcast(E5), lhsT_scale=q[1][:, j * P:(j + 1) * P],
+                                rhs=w_q[tb][0][:].bitcast(E4), rhs_scale=w_q[tb][1][:], start=(tb == 0), stop=(tb == TB - 1))
+
+        def w_pass(bank, tb, fb, nb):
+            q = tok_q[tb][nb]
+            nc.tensor.matmul_mx(out=bank[:], lhsT=x_q[nb][0][:, fb * P:(fb + 1) * P].bitcast(E4), lhsT_scale=x_q[nb][1][:, fb * P:(fb + 1) * P],
+                                rhs=q[0][:].bitcast(E5), rhs_scale=q[1][:], start=(nb == 0), stop=(nb == NB - 1))
+
+        def out_x_pair(nb, j0, engines):
+            st = stage_tile()
+            for i in range(2):
+                bank = bank_tile()
+                for tb in range(TB):
+                    x_pass(bank, nb, j0 + i, tb)
+                copy_on(engines[i], st[:, i, :], bank[:])
+                nc.sync.dma_start(out=o0_v[:, nb, j0 + i, :], in_=st[:, i, :])
+
+        def out_w_copy(tb, fb, eng, dst, bank):
+            copy_on(eng, dst, bank[:])
+            nc.sync.dma_start(out=o1_v[fb * P:(fb + 1) * P, :, tb * P:(tb + 1) * P], in_=dst.rearrange("f (l t) -> f l t", l=DEPTH))
+
+        def out_w_pair(tb, fb0, engines):
+            st = stage_tile()
+            for i in range(2):
+                bank = bank_tile()
+                for nb in range(NB):
+                    w_pass(bank, tb, fb0 + i, nb)
+                out_w_copy(tb, fb0 + i, engines[i], st[:, i, :], bank)
+
         tok_grp = {}
         feat_grp = {}
 
-        def stage_one(c, ahead, extra):
-            banks = list(ahead)
-            for k in range(16):
-                if k + 3 < 16:
-                    pass
-                weigh(k, banks[k])
-                if len(banks) < 16:
-                    banks.append(mx_group(c, len(banks)))
-                if k % 2 == 1 and c + 1 < len(chunks):
-                    make_pi(nc.gpsimd, k // 2)
-                for f in extra.get(k, ()):
-                    f()
-
-        def feat_quant(c):
+        def feat_quantize(c):
             tb, nb = chunks[c]
             quantize(feat_q[tb][nb], 0, N, feat_grp[c][:], E5)
 
-        def tok_quant(c):
+        def tok_quantize(c):
             tb, nb = chunks[c]
             quantize(tok_q[tb][nb], 0, N, tok_grp[c][:], E5)
 
-        def tail_phase(c, block, fills, vfills):
-            last = c + 1 == len(chunks)
+        def sum_chunk(c, extras):
             tb, nb = chunks[c]
-            dz = work.tile([P, PACK, DEPTH, P], BF16, name="dz", tag="dz", bufs=2)
-            grp = work.tile([P, 2048], BF16, name="fgrp", tag="fgrp", bufs=1, align_bytes=64)
+            dz = work.tile([P, PACK, DEPTH, P], BF16, name="dz", tag="dz", bufs=1)
+            grp = work.tile([P, PACK * 512], BF16, name="fgrp", tag="fgrp", bufs=1, align_bytes=64)
             feat_grp[c] = grp
-            A, Bk, M1, R, M2 = {}, {}, {}, {}, {}
+            rises, bases, scaled, sums, shares = {}, {}, {}, {}, {}
 
-            def p_tok(j, l0, l1):
-                return rz[c][j // 2][:, (j % 2) * DEPTH + l0:(j % 2) * DEPTH + l1, :]
+            def gate_of(j, l0, l1):
+                return z_raw[c][j // 2][:, (j % 2) * DEPTH + l0:(j % 2) * DEPTH + l1, :]
 
-            def m1(j):
-                M1[j] = tmp_tile(4)
-                nc.vector.scalar_tensor_tensor(out=M1[j][:], in0=A[j][:], scalar=INV_T, in1=p_tok(j, 3, 4).to_broadcast([P, 4, P]),
-                                               op0=ALU.mult, op1=ALU.mult)
+            def new_tile(n):
+                return work.tile([P, n, P], F32, name="tmp", tag="tmp", bufs=4)
 
-            def dzw(j):
-                nc.vector.scalar_tensor_tensor(out=dz[:, j, 3, :], in0=A[j][:, 0, :], scalar=INV_T, in1=stok[c][j // 2][:, j % 2, :],
-                                               op0=ALU.mult, op1=ALU.mult)
+            def scale_rise(j):
+                scaled[j] = new_tile(4)
+                nc.vector.scalar_tensor_tensor(out=scaled[j][:], in0=rises[j][:], scalar=INV_T,
+                                               in1=gate_of(j, 3, 4).to_broadcast([P, 4, P]), op0=ALU.mult, op1=ALU.mult)
 
-            def r(j):
-                R[j] = tmp_tile(4)
-                nc.vector.scalar_tensor_tensor(out=R[j][:], in0=Bk[j][:], scalar=INV_T, in1=M1[j][:], op0=ALU.mult, op1=ALU.add)
+            def dz_of_level_3(j):
+                nc.gpsimd.tensor_tensor(out=dz[:, j, 3, :], in0=scaled[j][:, 0, :], in1=qtok[c][j // 2][:, j % 2, :], op=ALU.mult)
 
-            def m2(j):
-                M2[j] = tmp_tile(3)
-                nc.vector.tensor_tensor(out=M2[j][:], in0=p_tok(j, 0, 3), in1=R[j][:, 0:1, :].to_broadcast([P, 3, P]), op=ALU.mult)
+            def add_base(j):
+                sums[j] = new_tile(4)
+                nc.vector.scalar_tensor_tensor(out=sums[j][:], in0=bases[j][:], scalar=INV_T, in1=scaled[j][:], op0=ALU.mult, op1=ALU.add)
 
-            def sub(j):
-                nc.vector.tensor_tensor(out=dz[:, j, 0:3, :], in0=R[j][:, 1:4, :], in1=M2[j][:], op=ALU.subtract)
+            def take_share(j):
+                shares[j] = new_tile(3)
+                nc.vector.tensor_tensor(out=shares[j][:], in0=gate_of(j, 0, 3), in1=sums[j][:, 0:1, :].to_broadcast([P, 3, P]), op=ALU.mult)
 
-            def run(fs, i):
-                for f in fs.get(i, ()):
+            def dz_of_levels_0_to_2(j):
+                nc.vector.tensor_tensor(out=dz[:, j, 0:3, :], in0=sums[j][:, 1:4, :], in1=shares[j][:], op=ALU.subtract)
+
+            def for_pair(fs, j0):
+                for f in fs:
+                    f(j0)
+                    f(j0 + 1)
+
+            def run(place):
+                for f in extras.get(place, ()):
                     f()
 
-            A[0], A[1] = sum_pair(steps_a(), 0)
-            run(fills, 0)
-            nc.vector.tensor_tensor(out=nus[:], in0=nup[:], in1=nuq[:], op=ALU.add)
-            for f in block:
-                f()
-            Bk[0], Bk[1] = sum_pair(steps_b(), 0)
-            for f in (m1, dzw, r):
-                f(0)
-                f(1)
-            A[2], A[3] = sum_pair(steps_a(), 2)
-            run(fills, 1)
-            for f in (m2, sub):
-                f(0)
-                f(1)
-            Bk[2], Bk[3] = sum_pair(steps_b(), 2)
-            run(fills, 2)
-            run(vfills, 3)
-            for f in (m1, dzw, r, m2, sub):
-                f(2)
-                f(3)
-            for j in range(2):
-                turn(j, dz, grp, "s")
-                if last:
-                    quantize(feat_q[tb][nb], j * P, (j + 1) * P, grp[:, 512 * j:512 * (j + 1)], E5)
-            run(fills, 3)
-            run(fills, 4)
-            ahead = []
-            if not last:
-                ahead = [mx_group(c + 1, k) for k in range(3)]
-            turn(2, dz, grp, "s")
-            turn(3, dz, grp, "s")
-            tg = grp_tile()
-            tok_grp[c] = tg
-            dst = tg[:].rearrange("p (c t) -> p c t", t=4)
-            src = dz[:].rearrange("p j l t -> p j (l t)")
-            if not last:
-                interleave("s", dst, src)
+            def feat_quantize_tile(j):
+                quantize(feat_q[tb][nb], j * P, (j + 1) * P, grp[:, N * j:N * (j + 1)], E5)
+
+            rises[0], rises[1] = turned_sums(rise_terms, 0)
+            run("behind rises 0")
+            nc.vector.tensor_tensor(out=base_sum[:], in0=base_p[:, 0:SUMMED, :], in1=base_q[:, 0:SUMMED, :], op=ALU.add)
+            run("behind base_sum")
+            bases[0], bases[1] = turned_sums(base_terms, 0)
+            for_pair((scale_rise, dz_of_level_3, add_base), 0)
+            rises[2], rises[3] = turned_sums(rise_terms, 2)
+            run("behind rises 2")
+            for_pair((take_share, dz_of_levels_0_to_2), 0)
+            run("behind dz 0")
+            bases[2], bases[3] = turned_sums(base_terms, 2)
+            run("behind bases 2")
+            for_pair((scale_rise, dz_of_level_3, add_base), 2)
+            turn_dz(dz, grp, 0)
+            turn_dz(dz, grp, 1)
+            run("behind turn 1")
+            for_pair((take_share, dz_of_levels_0_to_2), 2)
+            run("behind dz 2")
+            banks = [leaf_group(c + 1, k) for k in range(AHEAD)] if c < last_chunk else []
+            turn_dz(dz, grp, 2)
+            turn_dz(dz, grp, 3)
+            run("behind turn 3")
+            tok_grp[c] = group_tile()
+            if c < last_chunk:
+                interleave("s", tok_grp[c], dz[:].rearrange("p j l t -> p j (l t)"))
+                return banks
+
+            feat_quantize_tile(0)
+            feat_quantize_tile(1)
+            interleave("v", tok_grp[c], dz[:].rearrange("p j l t -> p j (l t)"))
+            out_x_pair(nb, 0, "ss")
+            for fb in range(2):
+                bank = bank_tile()
+                banks.append(bank)
+                w_pass(bank, tb, fb, 0)
+            tok_quantize(c)
+            for fb in range(2):
+                w_pass(banks[fb], tb, fb, 1)
+            st = stage_tile()
+            for fb in range(2):
+                out_w_copy(tb, fb, "vs"[fb], st[:, fb, :], banks[fb])
+            feat_quantize_tile(2)
+            feat_quantize_tile(3)
+            out_w_pair(tb, 2, "vs")
+            out_x_pair(nb, 2, "vs")
+            return banks
+
+        grads = {0: g_turn(0, "vs")}
+        z_banks = []
+        for lev in range(3):
+            bank = bank_tile()
+            z_turn(0, lev, bank)
+            z_banks.append(bank)
+        for lev, which in ((0, 0), (1, 0), (2, 0), (2, 1)):
+            gate(lev, which, z_banks[lev])
+        leaves = {0: leaf_turn(0, 0)}
+        for lev in (1, 0):
+            gate(lev, 1, z_banks[lev])
+        g_quantize(0, grads[0])
+        for a in range(4):
+            make_first_weights(nc.gpsimd if a == 3 else nc.vector, a)
+            leaf_quantize(leaves[a])
+            if a < 3:
+                leaves[a + 1] = leaf_turn(0, a + 1)
             else:
-                interleave("v", dst[:, 0:256, :], src[:, :, 0:256])
-                interleave("s", dst[:, 256:512, :], src[:, :, 256:512])
-                for j in range(2, 4):
-                    quantize(feat_q[tb][nb], j * P, (j + 1) * P, grp[:, 512 * j:512 * (j + 1)], E5)
-                tok_quant(c)
-                for j in range(4):
-                    out_x_group(nb, j, "sv"[j % 2])
-                for fb in range(4):
-                    out_w_group(tb, fb, "sv"[fb % 2])
-            return ahead
+                make_gates(1, 0)
+                make_gates(1, 1)
+                make_weight01()
+                make_gates(1, 2)
+            if a > 0:
+                for k in range(4 * a - 4, 4 * a):
+                    weigh(0, k, leaf_group(0, k))
+        make_token_gates(0)
+        make_token_gates(1)
+        for k in range(12, 16):
+            weigh(0, k, leaf_group(0, k))
+        grads[1] = g_turn(1, "ss")
+        for a in range(4):
+            make_weights(1, a)
 
-        pend = {}
+        late_leaves = {}
+        x_grp = {}
+        w_grp = {}
 
-        def later(name, f):
+        def late_leaf_turn(part):
             def go():
-                pend[name] = f()
+                late_leaves[part] = leaf_turn(1, part)
             return go
 
-        def prep_next(c):
-            def alphas():
-                for a in range(4):
-                    make_alpha(nc.gpsimd, a)
+        def late_leaf_quantize(part):
+            return lambda: leaf_quantize(late_leaves[part])
 
-            def toks():
-                stok[c + 2] = prep_tok(rz[c + 2])
-            return (lambda: prep_pq(rz[c + 2], 0), lambda: prep_pq(rz[c + 2], 1), alphas, lambda: prep_pq(rz[c + 2], 2), toks)
+        def late_x_turn(nb):
+            def go():
+                x_grp[nb] = x_turn(nb)
+            return go
 
-        n0 = prep_next(0)
-        ahead = tail_phase(0, [lambda: g_quant(1, g_grp)],
-                           {0: [n0[0]], 1: [n0[1], n0[2]], 2: [later("l0", lambda: leaf_turn(1, 0, "ss"))], 3: [n0[3]], 4: [later("l1", lambda: leaf_turn(1, 1, "ss")), n0[4]]},
-                           {3: [lambda: leaf_quant(pend["l0"])]})
-        stage_one(1, ahead, {2: [later("x0", lambda: x_turn(0))], 6: [later("x1", lambda: x_turn(1))]})
-        n1 = prep_next(1)
-        ahead = tail_phase(1, [lambda: leaf_quant(pend["l1"]), lambda: feat_quant(0), lambda: tok_quant(0),
-                               lambda: quantize(x_q[0], 0, F, pend["x0"][:], E4), lambda: quantize(x_q[1], 0, F, pend["x1"][:], E4)],
-                           {0: [n1[0]], 1: [n1[1], n1[2]], 2: [later("l2", lambda: leaf_turn(1, 2, "ss"))], 3: [n1[3]], 4: [later("l3", lambda: leaf_turn(1, 3, "ss")), n1[4]]},
-                           {3: [lambda: leaf_quant(pend["l2"])]})
-        stage_one(2, ahead, {1: [lambda: leaf_quant(pend["l3"])]})
+        def late_w_turn(tb, fb):
+            def go():
+                if fb == 0:
+                    w_grp[tb] = group_tile()
+                w_turn(tb, fb, w_grp[tb])
+            return go
 
-        def w_turn(tb, fb):
-            if fb == 0:
-                pend["w%d" % tb] = grp_tile()
-            grp = pend["w%d" % tb]
-            bank = psum.tile([P, DEPTH, P], BF16, name="tr", tag="tr", bufs=2)
-            for lev in range(DEPTH):
-                nc.tensor.transpose(bank[:, lev, :], w_raw[fb // 2][:, fb % 2, lev, tb * P:(tb + 1) * P], ident_b[:])
-            nc.scalar.copy(out=grp[:, 512 * fb:512 * (fb + 1)].rearrange("t (f l) -> t f l", l=DEPTH), in_=bank[:].rearrange("t l f -> t f l"))
+        def late_gates(c, lev):
+            return lambda: make_gates(c, lev)
 
-        ahead = tail_phase(2, [lambda: feat_quant(1), lambda: tok_quant(1)],
-                           {0: [lambda: w_turn(0, 0), lambda: w_turn(0, 1)], 1: [lambda: w_turn(0, 2), lambda: w_turn(0, 3)],
-                            2: [lambda: w_turn(1, 0), lambda: w_turn(1, 1)], 3: [lambda: w_turn(1, 2), lambda: w_turn(1, 3)]},
-                           {3: [lambda: quantize(w_q[0], 0, F, pend["w0"][:], E4)]})
-        stage_one(3, ahead, {1: [lambda: quantize(w_q[1], 0, F, pend["w1"][:], E4), lambda: out_w_group(0, 0, "s")],
-                             3: [lambda: feat_quant(2), lambda: out_w_group(0, 1, "s")],
-                             5: [lambda: tok_quant(2), lambda: out_w_group(0, 2, "s")],
-                             7: [lambda: out_w_group(0, 3, "s")],
-                             9: [lambda: out_x_group(0, 0, "s")], 11: [lambda: out_x_group(0, 1, "s")],
-                             13: [lambda: out_x_group(0, 2, "s")], 15: [lambda: out_x_group(0, 3, "s")]})
-        tail_phase(3, [], {}, {})
+        def late_token_gates(c):
+            return lambda: make_token_gates(c)
+
+        def x_quantize(nb):
+            return lambda: quantize(x_q[nb], 0, F, x_grp[nb][:], E4)
+
+        def w_quantize(tb):
+            return lambda: quantize(w_q[tb], 0, F, w_grp[tb][:], E4)
+
+        banks = sum_chunk(0, {
+            "behind rises 0": [late_gates(2, 0)],
+            "behind base_sum": [lambda: g_quantize(1, grads[1])],
+            "behind rises 2": [late_gates(2, 1), late_leaf_turn(0)],
+            "behind dz 0": [late_leaf_quantize(0)],
+            "behind turn 1": [late_gates(2, 2)],
+            "behind dz 2": [make_weight01],
+            "behind turn 3": [late_leaf_turn(1)],
+        })
+        weigh_chunk(1, banks, {
+            2: [late_x_turn(0)],
+            9: [late_leaf_turn(2)],
+            11: [late_leaf_turn(3)],
+            13: [late_gates(3, 0)],
+            15: [late_gates(3, 1)],
+        })
+        banks = sum_chunk(1, {
+            "behind rises 0": [late_gates(3, 2), late_token_gates(2)],
+            "behind base_sum": [late_leaf_quantize(1), lambda: feat_quantize(0), lambda: tok_quantize(0), x_quantize(0), late_leaf_quantize(2)],
+            "behind dz 0": [late_leaf_quantize(3)],
+            "behind bases 2": [late_x_turn(1)],
+            "behind dz 2": [make_weight01],
+        })
+        weigh_chunk(2, banks, {8 + 4 * tb + fb: [late_w_turn(tb, fb)] for tb in range(TB) for fb in range(4)})
+        banks = sum_chunk(2, {
+            "behind rises 0": [late_token_gates(3)],
+            "behind base_sum": [lambda: feat_quantize(1), lambda: tok_quantize(1), x_quantize(1), w_quantize(0)],
+            "behind dz 0": [w_quantize(1)],
+        })
+        weigh_chunk(3, banks, {
+            5: [lambda: feat_quantize(2), lambda: out_w_pair(0, 0, "ss")],
+            9: [lambda: tok_quantize(2), lambda: out_w_pair(0, 2, "ss")],
+        })
+        sum_chunk(3, {"behind turn 1": [lambda: out_x_pair(0, 0, "ss"), lambda: out_x_pair(0, 2, "ss")]})

from contextlib import ExitStack

import concourse.mybir as mybir
from concourse.masks import make_identity

B, F, DEPTH, T, DO = 1024, 512, 4, 256, 512
L = 2 ** DEPTH
H = T * DEPTH

FLOPS = 2 * B * DO * T * L + 2 * 2 * B * F * H
BYTES = 2 * B * F + 2 * F * H + 2 * T * L * DO + 4 * B * H + 2 * B * DO + 4 * B * F + 4 * F * H

F32 = mybir.dt.float32
BF16 = mybir.dt.bfloat16
U32 = mybir.dt.uint32
U8 = mybir.dt.uint8
E4 = mybir.dt.float8_e4m3fn_x4
E5 = mybir.dt.float8_e5m2_x4
ALU = mybir.AluOpType
ACT = mybir.ActivationFunctionType

P = 128
PACK = 4
N = P * PACK
NB = B // N
TB = T // P
PAIRS = L // 2
AHEAD = 3
SUMMED = 3
INV_T = 1.0 / T


def tile_neuralobliviousdecisiontree_v_kernel(tc, x, W, b, leaf_values, z, grad_out, out_0, out_1):
    nc = tc.nc
    with ExitStack() as ctx:
        const = ctx.enter_context(tc.tile_pool(name="const", bufs=1))
        raw = ctx.enter_context(tc.tile_pool(name="raw", bufs=5))
        work = ctx.enter_context(tc.tile_pool(name="work", bufs=2))
        psum = ctx.enter_context(tc.psum_pool(name="psum", bufs=2))

        ident_f = const.tile([P, P], F32, name="ident_f")
        make_identity(nc, ident_f[:])
        ident_b = const.tile([P, P], BF16, name="ident_b")
        make_identity(nc, ident_b[:])

        ctx.enter_context(tc.manual_schedule())

        def codes_and_scales(name, cols):
            codes = const.tile([P, cols], U32, name=name + "_c", align_bytes=64)
            scales = const.tile([P, cols], U8, name=name + "_s", align_bytes=64)
            return codes, scales

        leaf_q = [codes_and_scales("leaf%d" % tb, L * P) for tb in range(TB)]
        gpos_q = [codes_and_scales("gpos%d" % nb, N) for nb in range(NB)]
        gneg_q = [codes_and_scales("gneg%d" % nb, N) for nb in range(NB)]
        x_q = [codes_and_scales("x%d" % nb, F) for nb in range(NB)]
        w_q = [codes_and_scales("w%d" % tb, F) for tb in range(TB)]
        tok_q = [[codes_and_scales("tok%d%d" % (tb, nb), N) for nb in range(NB)] for tb in range(TB)]
        feat_q = [[codes_and_scales("feat%d%d" % (tb, nb), N) for nb in range(NB)] for tb in range(TB)]
        rise = const.tile([P, PAIRS, N], F32, name="rise")
        base_p = const.tile([P, 4, N], F32, name="base_p")
        base_q = const.tile([P, 4, N], F32, name="base_q")
        base_sum = const.tile([P, SUMMED, N], F32, name="base_sum")
        weight01 = const.tile([P, 4, N], F32, name="weight01")
        gates = [const.tile([P, 2, N], F32, name="gates%d" % lev) for lev in range(3)]
        weights = {}
        qtok = {}

        z_v = z.rearrange("n l t -> (n l) t").rearrange("(g p m) t -> p g m t", p=P, m=PACK * DEPTH)
        g_v = grad_out.rearrange("(g p j) d -> p g j d", p=P, j=PACK)
        x_v = x.rearrange("(g p j) f -> p g j f", p=P, j=PACK)
        o0_v = out_0.rearrange("(g p j) f -> p g j f", p=P, j=PACK)
        w_v = W.rearrange("l (b p) t -> p b l t", p=P)
        o1_v = out_1.rearrange("l f t -> f l t")
        chunks = [(tb, nb) for tb in range(TB) for nb in range(NB)]
        last_chunk = len(chunks) - 1

        def load_z(c):
            tb, nb = chunks[c]
            tiles = []
            for h in range(2):
                t = raw.tile([P, 2 * DEPTH, P], F32, name="ztile", tag="ztile", bufs=6)
                nc.sync.dma_start(out=t[:], in_=z_v[:, nb, 8 * h:8 * h + 8, tb * P:(tb + 1) * P])
                tiles.append(t)
            return tiles

        def load_tokens(view, nb):
            t = raw.tile([P, PACK, 512], BF16, name="raw", tag="raw")
            nc.sync.dma_start(out=t[:], in_=view[:, nb, :, :])
            return t

        def load_leaves(tb, part):
            t = raw.tile([P, 4, DO], BF16, name="raw", tag="raw")
            nc.sync.dma_start(out=t[:], in_=leaf_values[tb * P:(tb + 1) * P, 4 * part:4 * part + 4, :])
            return t

        def load_w(half):
            t = raw.tile([P, 2, DEPTH, T], BF16, name="raw", tag="raw")
            for i in range(2):
                nc.sync.dma_start(out=t[:, i, :, :], in_=w_v[:, 2 * half + i, :, :])
            return t

        g_raw = [load_tokens(g_v, 0)]
        z_raw = [load_z(0)]
        leaf_raw = {}
        for part in range(4):
            leaf_raw[0, part] = load_leaves(0, part)
        z_raw.append(load_z(1))
        g_raw.append(load_tokens(g_v, 1))
        z_raw.append(load_z(2))
        for part in range(4):
            leaf_raw[1, part] = load_leaves(1, part)
        x_raw = [load_tokens(x_v, nb) for nb in range(NB)]
        z_raw.append(load_z(3))
        w_raw = [load_w(half) for half in range(2)]

        def quantize(q, c0, c1, src, fmt):
            nc.vector.quantize_mx(out=q[0][:, c0:c1].bitcast(fmt), scales=q[1][:, c0:c1], in_=src)

        def copy_on(eng, dst, src):
            if eng == "v":
                nc.vector.tensor_copy(out=dst, in_=src)
            else:
                nc.scalar.copy(out=dst, in_=src)

        def group_tile():
            return work.tile([P, PACK * 512], BF16, name="grp", tag="grp", bufs=4, align_bytes=64)

        def bank_tile():
            return psum.tile([P, N], F32, name="bank", tag="bank", bufs=6)

        def turn_rows(dst, rows_a, rows_b, eng):
            bank = psum.tile([P, 2, 2, P], F32, name="turned", tag="turned", bufs=2)
            for i, rows in enumerate((rows_a, rows_b)):
                words = rows.bitcast(F32)
                for u in range(2):
                    nc.tensor.transpose(bank[:, i, u, :], words[:, u:256:2], ident_f[:])
            copy_on(eng, dst.bitcast(F32).rearrange("k (i r u) -> k i r u", i=2, u=2), bank[:].rearrange("k i u r -> k i r u"))

        def leaf_turn(tb, part):
            out = []
            for i in range(2):
                grp = work.tile([P, 2 * P * PACK], BF16, name="lgrp", tag="lgrp", bufs=4, align_bytes=64)
                t = leaf_raw[tb, part]
                turn_rows(grp[:], t[:, 2 * i, :], t[:, 2 * i + 1, :], "s")
                out.append((tb, 4 * part + 2 * i, grp))
            return out

        def leaf_quantize(items):
            for tb, leaf, grp in items:
                quantize(leaf_q[tb], leaf * P, (leaf + 2) * P, grp[:], E4)

        def g_turn(nb, engines):
            grp = group_tile()
            for i in range(2):
                turn_rows(grp[:, 1024 * i:1024 * (i + 1)], g_raw[nb][:, 2 * i, :], g_raw[nb][:, 2 * i + 1, :], engines[i])
            return grp

        def g_quantize(nb, grp):
            neg = group_tile()
            nc.vector.tensor_scalar_mul(neg[:], grp[:], -1.0)
            quantize(gpos_q[nb], 0, N, grp[:], E5)
            quantize(gneg_q[nb], 0, N, neg[:], E5)

        def interleave(eng, grp, src):
            dst = grp[:].rearrange("p (c i j) -> p c j i", i=4, j=PACK)
            copy_on(eng, dst, src.rearrange("p j (c i) -> p c j i", i=4))

        def x_turn(nb):
            grp = group_tile()
            interleave("s", grp, x_raw[nb][:])
            return grp

        def w_turn(tb, fb, grp):
            bank = psum.tile([P, DEPTH, P], BF16, name="turned", tag="turned", bufs=2)
            for lev in range(DEPTH):
                nc.tensor.transpose(bank[:, lev, :], w_raw[fb // 2][:, fb % 2, lev, tb * P:(tb + 1) * P], ident_b[:])
            nc.scalar.copy(out=grp[:, N * fb:N * (fb + 1)].rearrange("t (f l) -> t f l", l=DEPTH), in_=bank[:].rearrange("t l f -> t f l"))

        def z_turn(c, lev, bank):
            for j in range(PACK):
                nc.tensor.transpose(bank[:, j * P:(j + 1) * P], z_raw[c][j // 2][:, (j % 2) * DEPTH + lev, :], ident_f[:])

        def gate(lev, which, bank):
            nc.scalar.activation(out=gates[lev][:, which, :], in_=bank[:], func=ACT.Sigmoid, scale=-1.0 if which else 1.0)

        def make_gates(c, lev):
            bank = psum.tile([P, N], F32, name="turned", tag="turned", bufs=2)
            z_turn(c, lev, bank)
            gate(lev, 0, bank)
            gate(lev, 1, bank)

        def make_token_gates(c):
            qtok[c] = []
            for h in range(2):
                t = work.tile([P, 2, P], F32, name="qtok", tag="qtok", bufs=4)
                nc.scalar.activation(out=t[:], in_=z_raw[c][h][:, 3:2 * DEPTH:DEPTH, :], func=ACT.Sigmoid, scale=-1.0)
                nc.scalar.activation(out=z_raw[c][h][:], in_=z_raw[c][h][:], func=ACT.Sigmoid)
                qtok[c].append(t)

        def make_weight01():
            for i in range(2):
                nc.vector.tensor_tensor(out=weight01[:, 2 * i:2 * i + 2, :], in0=gates[0][:, i:i + 1, :].to_broadcast([P, 2, N]),
                                        in1=gates[1][:], op=ALU.mult)

        def weight_tile(c, a):
            weights[c, a] = work.tile([P, 2, N], F32, name="weight", tag="weight", bufs=7)
            return weights[c, a]

        def make_weights(c, a):
            t = weight_tile(c, a)
            nc.gpsimd.tensor_tensor(out=t[:], in0=weight01[:, a:a + 1, :].to_broadcast([P, 2, N]), in1=gates[2][:], op=ALU.mult)

        def make_first_weights(eng, a):
            eng.tensor_tensor(out=weight01[:, a, :], in0=gates[0][:, a // 2, :], in1=gates[1][:, a % 2, :], op=ALU.mult)
            t = weight_tile(0, a)
            for i in range(2):
                eng.tensor_tensor(out=t[:, i, :], in0=weight01[:, a, :], in1=gates[2][:, i, :], op=ALU.mult)

        def leaf_pass(bank, tb, leaf, q, start, stop):
            nc.tensor.matmul_mx(out=bank[:], lhsT=leaf_q[tb][0][:, leaf * P:(leaf + 1) * P].bitcast(E4),
                                lhsT_scale=leaf_q[tb][1][:, leaf * P:(leaf + 1) * P],
                                rhs=q[0][:].bitcast(E5), rhs_scale=q[1][:], start=start, stop=stop)

        def leaf_group(c, k):
            tb, nb = chunks[c]
            bank = bank_tile()
            if k % 2:
                leaf_pass(bank, tb, k, gpos_q[nb], True, True)
            else:
                leaf_pass(bank, tb, k, gpos_q[nb], True, False)
                leaf_pass(bank, tb, k + 1, gneg_q[nb], False, True)
            return bank

        def weigh(c, k, bank):
            a, odd = k // 4, (k // 2) % 2
            if k % 2 == 0:
                dst = rise[:, k // 2, :]
            else:
                dst = base_q[:, a, :] if odd else base_p[:, a, :]
            nc.vector.tensor_tensor(out=dst, in0=bank[:], in1=weights[c, a][:, odd, :], op=ALU.mult)

        def weigh_chunk(c, banks, extras):
            for k in range(2 * PAIRS):
                if k % 4 == 0 and c < last_chunk:
                    make_weights(c + 1, k // 4)
                weigh(c, k, banks[k])
                if len(banks) < 2 * PAIRS:
                    banks.append(leaf_group(c, len(banks)))
                for f in extras.get(k, ()):
                    f()

        rise_terms = []
        for s, chosen in enumerate((range(8), range(4), (0, 1, 4, 5), (0, 2, 4, 6))):
            rise_terms.append((s, [(rise, i) for i in chosen]))
        base_terms = [(3, [(base_p, a) for a in range(4)])]
        for s, chosen in enumerate((range(4), (0, 1), (0, 2))):
            terms = []
            for a in chosen:
                terms.extend([(base_sum, a)] if a < SUMMED else [(base_p, a), (base_q, a)])
            base_terms.append((s, terms))

        def turned_sums(sums, j0):
            banks = []
            for j in range(2):
                bank = psum.tile([P, 4, P], F32, name="bank", tag="bank", bufs=6)
                banks.append(bank)
            for s, terms in sums:
                for n, (src, i) in enumerate(terms):
                    for j in range(2):
                        nc.tensor.matmul(banks[j][:, s, :], lhsT=src[:, i, (j0 + j) * P:(j0 + j + 1) * P], rhs=ident_f[:],
                                         start=(n == 0), stop=(n + 1 == len(terms)), is_transpose=True)
            return banks

        def turn_dz(dz, grp, j):
            bank = psum.tile([P, DEPTH, P], BF16, name="turned", tag="turned", bufs=2)
            for lev in range(DEPTH):
                nc.tensor.transpose(bank[:, lev, :], dz[:, j, lev, :], ident_b[:])
            nc.scalar.copy(out=grp[:, N * j:N * (j + 1)].rearrange("t (p l) -> t p l", l=DEPTH), in_=bank[:].rearrange("t l p -> t p l"))

        def stage_tile():
            return raw.tile([P, 2, N], F32, name="ztile", tag="ztile", bufs=6)

        def x_pass(bank, nb, j, tb):
            q = feat_q[tb][nb]
            nc.tensor.matmul_mx(out=bank[:], lhsT=q[0][:, j * P:(j + 1) * P].bitcast(E5), lhsT_scale=q[1][:, j * P:(j + 1) * P],
                                rhs=w_q[tb][0][:].bitcast(E4), rhs_scale=w_q[tb][1][:], start=(tb == 0), stop=(tb == TB - 1))

        def w_pass(bank, tb, fb, nb):
            q = tok_q[tb][nb]
            nc.tensor.matmul_mx(out=bank[:], lhsT=x_q[nb][0][:, fb * P:(fb + 1) * P].bitcast(E4), lhsT_scale=x_q[nb][1][:, fb * P:(fb + 1) * P],
                                rhs=q[0][:].bitcast(E5), rhs_scale=q[1][:], start=(nb == 0), stop=(nb == NB - 1))

        def out_x_pair(nb, j0, engines):
            st = stage_tile()
            for i in range(2):
                bank = bank_tile()
                for tb in range(TB):
                    x_pass(bank, nb, j0 + i, tb)
                copy_on(engines[i], st[:, i, :], bank[:])
                nc.sync.dma_start(out=o0_v[:, nb, j0 + i, :], in_=st[:, i, :])

        def out_w_copy(tb, fb, eng, dst, bank):
            copy_on(eng, dst, bank[:])
            nc.sync.dma_start(out=o1_v[fb * P:(fb + 1) * P, :, tb * P:(tb + 1) * P], in_=dst.rearrange("f (l t) -> f l t", l=DEPTH))

        def out_w_pair(tb, fb0, engines):
            st = stage_tile()
            for i in range(2):
                bank = bank_tile()
                for nb in range(NB):
                    w_pass(bank, tb, fb0 + i, nb)
                out_w_copy(tb, fb0 + i, engines[i], st[:, i, :], bank)

        tok_grp = {}
        feat_grp = {}

        def feat_quantize(c):
            tb, nb = chunks[c]
            quantize(feat_q[tb][nb], 0, N, feat_grp[c][:], E5)

        def tok_quantize(c):
            tb, nb = chunks[c]
            quantize(tok_q[tb][nb], 0, N, tok_grp[c][:], E5)

        def sum_chunk(c, extras):
            tb, nb = chunks[c]
            dz = work.tile([P, PACK, DEPTH, P], BF16, name="dz", tag="dz", bufs=1)
            grp = work.tile([P, PACK * 512], BF16, name="fgrp", tag="fgrp", bufs=1, align_bytes=64)
            feat_grp[c] = grp
            rises, bases, scaled, sums, shares = {}, {}, {}, {}, {}

            def gate_of(j, l0, l1):
                return z_raw[c][j // 2][:, (j % 2) * DEPTH + l0:(j % 2) * DEPTH + l1, :]

            def new_tile(n):
                return work.tile([P, n, P], F32, name="tmp", tag="tmp", bufs=4)

            def scale_rise(j):
                scaled[j] = new_tile(4)
                nc.vector.scalar_tensor_tensor(out=scaled[j][:], in0=rises[j][:], scalar=INV_T,
                                               in1=gate_of(j, 3, 4).to_broadcast([P, 4, P]), op0=ALU.mult, op1=ALU.mult)

            def dz_of_level_3(j):
                nc.gpsimd.tensor_tensor(out=dz[:, j, 3, :], in0=scaled[j][:, 0, :], in1=qtok[c][j // 2][:, j % 2, :], op=ALU.mult)

            def add_base(j):
                sums[j] = new_tile(4)
                nc.vector.scalar_tensor_tensor(out=sums[j][:], in0=bases[j][:], scalar=INV_T, in1=scaled[j][:], op0=ALU.mult, op1=ALU.add)

            def take_share(j):
                shares[j] = new_tile(3)
                nc.vector.tensor_tensor(out=shares[j][:], in0=gate_of(j, 0, 3), in1=sums[j][:, 0:1, :].to_broadcast([P, 3, P]), op=ALU.mult)

            def dz_of_levels_0_to_2(j):
                nc.vector.tensor_tensor(out=dz[:, j, 0:3, :], in0=sums[j][:, 1:4, :], in1=shares[j][:], op=ALU.subtract)

            def for_pair(fs, j0):
                for f in fs:
                    f(j0)
                    f(j0 + 1)

            def run(place):
                for f in extras.get(place, ()):
                    f()

            def feat_quantize_tile(j):
                quantize(feat_q[tb][nb], j * P, (j + 1) * P, grp[:, N * j:N * (j + 1)], E5)

            rises[0], rises[1] = turned_sums(rise_terms, 0)
            run("behind rises 0")
            nc.vector.tensor_tensor(out=base_sum[:], in0=base_p[:, 0:SUMMED, :], in1=base_q[:, 0:SUMMED, :], op=ALU.add)
            run("behind base_sum")
            bases[0], bases[1] = turned_sums(base_terms, 0)
            for_pair((scale_rise, dz_of_level_3, add_base), 0)
            rises[2], rises[3] = turned_sums(rise_terms, 2)
            run("behind rises 2")
            for_pair((take_share, dz_of_levels_0_to_2), 0)
            run("behind dz 0")
            bases[2], bases[3] = turned_sums(base_terms, 2)
            run("behind bases 2")
            for_pair((scale_rise, dz_of_level_3, add_base), 2)
            turn_dz(dz, grp, 0)
            turn_dz(dz, grp, 1)
            run("behind turn 1")
            for_pair((take_share, dz_of_levels_0_to_2), 2)
            run("behind dz 2")
            banks = [leaf_group(c + 1, k) for k in range(AHEAD)] if c < last_chunk else []
            turn_dz(dz, grp, 2)
            turn_dz(dz, grp, 3)
            run("behind turn 3")
            tok_grp[c] = group_tile()
            if c < last_chunk:
                interleave("s", tok_grp[c], dz[:].rearrange("p j l t -> p j (l t)"))
                return banks

            feat_quantize_tile(0)
            feat_quantize_tile(1)
            interleave("v", tok_grp[c], dz[:].rearrange("p j l t -> p j (l t)"))
            out_x_pair(nb, 0, "ss")
            for fb in range(2):
                bank = bank_tile()
                banks.append(bank)
                w_pass(bank, tb, fb, 0)
            tok_quantize(c)
            for fb in range(2):
                w_pass(banks[fb], tb, fb, 1)
            st = stage_tile()
            for fb in range(2):
                out_w_copy(tb, fb, "vs"[fb], st[:, fb, :], banks[fb])
            feat_quantize_tile(2)
            feat_quantize_tile(3)
            out_w_pair(tb, 2, "vs")
            out_x_pair(nb, 2, "vs")
            return banks

        grads = {0: g_turn(0, "vs")}
        z_banks = []
        for lev in range(3):
            bank = bank_tile()
            z_turn(0, lev, bank)
            z_banks.append(bank)
        for lev, which in ((0, 0), (1, 0), (2, 0), (2, 1)):
            gate(lev, which, z_banks[lev])
        leaves = {0: leaf_turn(0, 0)}
        for lev in (1, 0):
            gate(lev, 1, z_banks[lev])
        g_quantize(0, grads[0])
        for a in range(4):
            make_first_weights(nc.gpsimd if a == 3 else nc.vector, a)
            leaf_quantize(leaves[a])
            if a < 3:
                leaves[a + 1] = leaf_turn(0, a + 1)
            else:
                make_gates(1, 0)
                make_gates(1, 1)
                make_weight01()
                make_gates(1, 2)
            if a > 0:
                for k in range(4 * a - 4, 4 * a):
                    weigh(0, k, leaf_group(0, k))
        make_token_gates(0)
        make_token_gates(1)
        for k in range(12, 16):
            weigh(0, k, leaf_group(0, k))
        grads[1] = g_turn(1, "ss")
        for a in range(4):
            make_weights(1, a)

        late_leaves = {}
        x_grp = {}
        w_grp = {}

        def late_leaf_turn(part):
            def go():
                late_leaves[part] = leaf_turn(1, part)
            return go

        def late_leaf_quantize(part):
            return lambda: leaf_quantize(late_leaves[part])

        def late_x_turn(nb):
            def go():
                x_grp[nb] = x_turn(nb)
            return go

        def late_w_turn(tb, fb):
            def go():
                if fb == 0:
                    w_grp[tb] = group_tile()
                w_turn(tb, fb, w_grp[tb])
            return go

        def late_gates(c, lev):
            return lambda: make_gates(c, lev)

        def late_token_gates(c):
            return lambda: make_token_gates(c)

        def x_quantize(nb):
            return lambda: quantize(x_q[nb], 0, F, x_grp[nb][:], E4)

        def w_quantize(tb):
            return lambda: quantize(w_q[tb], 0, F, w_grp[tb][:], E4)

        banks = sum_chunk(0, {
            "behind rises 0": [late_gates(2, 0)],
            "behind base_sum": [lambda: g_quantize(1, grads[1])],
            "behind rises 2": [late_gates(2, 1), late_leaf_turn(0)],
            "behind dz 0": [late_leaf_quantize(0)],
            "behind turn 1": [late_gates(2, 2)],
            "behind dz 2": [make_weight01],
            "behind turn 3": [late_leaf_turn(1)],
        })
        weigh_chunk(1, banks, {
            2: [late_x_turn(0)],
            9: [late_leaf_turn(2)],
            11: [late_leaf_turn(3)],
            13: [late_gates(3, 0)],
            15: [late_gates(3, 1)],
        })
        banks = sum_chunk(1, {
            "behind rises 0": [late_gates(3, 2), late_token_gates(2)],
            "behind base_sum": [late_leaf_quantize(1), lambda: feat_quantize(0), lambda: tok_quantize(0), x_quantize(0), late_leaf_quantize(2)],
            "behind dz 0": [late_leaf_quantize(3)],
            "behind bases 2": [late_x_turn(1)],
            "behind dz 2": [make_weight01],
        })
        weigh_chunk(2, banks, {8 + 4 * tb + fb: [late_w_turn(tb, fb)] for tb in range(TB) for fb in range(4)})
        banks = sum_chunk(2, {
            "behind rises 0": [late_token_gates(3)],
            "behind base_sum": [lambda: feat_quantize(1), lambda: tok_quantize(1), x_quantize(1), w_quantize(0)],
            "behind dz 0": [w_quantize(1)],
        })
        weigh_chunk(3, banks, {
            5: [lambda: feat_quantize(2), lambda: out_w_pair(0, 0, "ss")],
            9: [lambda: tok_quantize(2), lambda: out_w_pair(0, 2, "ss")],
        })
        sum_chunk(3, {"behind turn 1": [lambda: out_x_pair(0, 0, "ss"), lambda: out_x_pair(0, 2, "ss")]})
